import numpy as np
import ml_dtypes


def mxq(x, axis, fmt="e4m3"):
    dtype, down = {"e4m3": (ml_dtypes.float8_e4m3fn, 7), "e5m2": (ml_dtypes.float8_e5m2, 14)}[fmt]
    v = np.moveaxis(np.asarray(x, np.float32).astype(ml_dtypes.bfloat16).astype(np.float64), axis, -1)
    blocks = v.reshape(v.shape[:-1] + (-1, 32))
    amax = np.abs(blocks).max(-1, keepdims=True)
    byte = np.maximum(np.where(amax > 0, np.frexp(amax)[1] - 1 + 127, 0) - down, 1)
    scale = np.exp2(byte - 127.0)
    codes = (blocks / scale).astype(np.float32).astype(dtype).astype(np.float64)
    return np.moveaxis((codes * scale).reshape(v.shape), -1, axis)


WIDE = False


def mx_kscale(k):
    if not WIDE:
        return np.ones(k)
    levels = np.array([10, -10, 5, -5, 0])
    if k % 512:
        return np.exp2(np.random.permutation(np.resize(levels, k // 32))).repeat(32)
    a = np.empty((k // 512, 16))
    for p in range(k // 512):
        a[p, :8] = np.random.permutation(np.resize(levels, 8))
        for g in range(8):
            far = levels[np.abs(levels - a[p, g]) >= 10]
            a[p, g + 8] = far[np.random.randint(len(far))]
    return np.exp2(a.ravel()).repeat(32)


BF16 = ml_dtypes.bfloat16


def bf(x):
    return np.asarray(x, np.float32).astype(BF16)


def f64(x):
    return np.asarray(x).astype(np.float64)


B, S, D, NH, NKV, HD = 2, 256, 2048, 16, 4, 128
EPS = 1e-6
QS = NH * HD
KS = NKV * HD
E = QS + KS + KS
HP = HD // 2


def rmsnorm(v, w):
    ms = np.mean(np.square(v), axis=-1, keepdims=True)
    return v * (1.0 / np.sqrt(ms + EPS)) * w


def apply_rotary_emb(v, fc):
    vs = v.reshape(*v.shape[:-1], HP, 2)
    f = fc[None, :, None, :, :]
    vr, vi = vs[..., 0], vs[..., 1]
    fr, fi = f[..., 0], f[..., 1]
    return np.stack([vr * fr - vi * fi, vi * fr + vr * fi], axis=-1).reshape(v.shape)


def draw0():
    s = mx_kscale(D)
    return {"x": bf(np.random.standard_normal((B, S, D)) * s),
            "freqs_cis": bf(np.random.standard_normal((S, HP, 2))),
            "wqkv": bf(np.random.standard_normal((E, D)) / np.sqrt(D) / s[None, :]),
            "q_norm_w": bf(1.0 + 0.1 * np.random.standard_normal(HD)),
            "k_norm_w": bf(1.0 + 0.1 * np.random.standard_normal(HD))}


def core(x, freqs_cis, wqkv, q_norm_w, k_norm_w):
    fc = f64(freqs_cis)
    qkv = mxq(f64(x), 2, "e4m3") @ mxq(f64(wqkv), 1, "e4m3").T
    q = qkv[..., :QS].reshape(B, S, NH, HD)
    k = qkv[..., QS:QS + KS].reshape(B, S, NKV, HD)
    v = qkv[..., QS + KS:].reshape(B, S, NKV, HD)
    q = rmsnorm(q, f64(q_norm_w))
    k = rmsnorm(k, f64(k_norm_w))
    q_rot = apply_rotary_emb(q, fc)
    k_rot = apply_rotary_emb(k, fc)
    return q_rot, k_rot, v


def e4m3fn_bytes(y):
    return np.clip(np.asarray(y, np.float64), -448.0, 448.0).astype(np.float32).astype(ml_dtypes.float8_e4m3fn).view(np.uint8)


def e4m3fn_values(b):
    return np.asarray(b, np.uint8).view(ml_dtypes.float8_e4m3fn).astype(np.float64)


def setup_inputs():
    d = draw0()
    x0 = np.asarray(d['wqkv']).astype(np.float64)
    s = (np.max(np.abs(x0), axis=(0,), keepdims=True) / 448.0).astype(np.float32)
    out = {}
    for k, v in d.items():
        if k == 'wqkv':
            out['wqkv_bytes'] = e4m3fn_bytes(x0 / s.astype(np.float64))
            out['wqkv_scale'] = s
        else:
            out[k] = v
    return out


def reference(x, freqs_cis, wqkv_bytes, wqkv_scale, q_norm_w, k_norm_w):
    return core(x, freqs_cis, e4m3fn_values(wqkv_bytes) * wqkv_scale.astype(np.float64), q_norm_w, k_norm_w)

@@ -1,0 +1,352 @@
+from contextlib import ExitStack
+
+import concourse.mybir as mybir
+from concourse.masks import make_identity
+
+FLOPS = 2 * 512 * 3072 * 2048
+
+F32 = mybir.dt.float32
+BF16 = mybir.dt.bfloat16
+U32 = mybir.dt.uint32
+U8 = mybir.dt.uint8
+FP8 = mybir.dt.float8_e4m3fn
+FP8X4 = mybir.dt.float8_e4m3fn_x4
+ALU = mybir.AluOpType
+ACT = mybir.ActivationFunctionType
+
+P = 128
+D = 2048
+PASSES = 4
+TOK_TILES = 4
+ROW_TILES = 24
+GROUPS = 6
+ROPE_GROUPS = 5
+UNITS = 4 + 4 * GROUPS
+EPS = 1e-6
+MANUAL = True
+S_PASSES = (2, 3, 2, 2, 2, 0)
+
+
+def tile_attention_pa_kernel(tc, x, freqs_cis, wqkv_bytes, wqkv_scale, q_norm_w, k_norm_w, out_0, out_1, out_2):
+    nc = tc.nc
+    x_rows = x.rearrange("b s d -> (b s) d").rearrange("(m p) d -> p m d", p=P)
+    outs = [
+        out_0.rearrange("b s h d -> (b s) (h d)"),
+        out_1.rearrange("b s h d -> (b s) (h d)"),
+        out_2.rearrange("b s h d -> (b s) (h d)"),
+    ]
+
+    with ExitStack() as ctx:
+        keep = ctx.enter_context(tc.tile_pool(name="keep", bufs=1))
+        bytes_pool = ctx.enter_context(tc.tile_pool(name="bytes_pool", bufs=ROW_TILES))
+        wide_pool = ctx.enter_context(tc.tile_pool(name="wide_pool", bufs=10))
+        cast_pool = ctx.enter_context(tc.tile_pool(name="cast_pool", bufs=2))
+        grouped_pool = ctx.enter_context(tc.tile_pool(name="grouped_pool", bufs=5))
+        codes_pool = ctx.enter_context(tc.tile_pool(name="codes_pool", bufs=3))
+        rope_pool = ctx.enter_context(tc.tile_pool(name="rope_pool", bufs=4))
+        out_pool = ctx.enter_context(tc.tile_pool(name="out_pool", bufs=6))
+        stat_pool = ctx.enter_context(tc.tile_pool(name="stat_pool", bufs=2))
+        psum_t = ctx.enter_context(tc.psum_pool(name="psum_t", bufs=4))
+        psum_acc = ctx.enter_context(tc.psum_pool(name="psum_acc", bufs=4))
+        if MANUAL:
+            ctx.enter_context(tc.manual_schedule())
+
+        fc = keep.tile([P, 2, 64, 2], BF16, name="fc")
+        nc.scalar.dma_start(out=fc[:].rearrange("p t j e -> p t (j e)"), in_=freqs_cis.rearrange("(t p) j e -> p t (j e)", p=P))
+        gains = []
+        for name, vec in (("gain_q", q_norm_w), ("gain_k", k_norm_w)):
+            g_t = keep.tile([P, 128], BF16, name=name)
+            nc.scalar.dma_start(out=g_t[:], in_=vec.partition_broadcast(P))
+            gains.append(g_t)
+        scale_b = keep.tile([P, D], F32, name="scale_b")
+        scale_row = wqkv_scale.rearrange("o k -> (o k)")
+        for c in range(4):
+            nc.scalar.dma_start(out=scale_b[:, 512 * c : 512 * (c + 1)], in_=scale_row[512 * c : 512 * (c + 1)].partition_broadcast(P))
+
+        scale_col = keep.tile([P, 16], F32, name="scale_col")
+        nc.scalar.dma_start(out=scale_col[:].rearrange("p (g t) -> p g t", t=4), in_=wqkv_scale.rearrange("o (g p t) -> p (o g) t", p=P, t=4))
+
+        w_bytes = []
+        x_raw = []
+
+        def load_w(t):
+            wb = bytes_pool.tile([P, D], U8, name="w_bytes_%d" % t, tag="w_bytes")
+            nc.sync.dma_start(out=wb[:], in_=wqkv_bytes[P * t : P * (t + 1), :])
+            w_bytes.append(wb)
+
+        def load_x(c):
+            xr = keep.tile([P, TOK_TILES, 512], BF16, name="x_raw_%d" % c)
+            nc.sync.dma_start(out=xr[:], in_=x_rows[:, :, 512 * c : 512 * (c + 1)])
+            x_raw.append(xr)
+
+        load_w(0)
+        load_x(0)
+        load_w(1)
+        load_x(1)
+        load_x(2)
+        load_w(2)
+        load_x(3)
+        for t in range(3, ROW_TILES):
+            load_w(t)
+
+        ident = keep.tile([P, P], F32, name="ident")
+        make_identity(nc, ident[:])
+        ident_bf = keep.tile([P, P], BF16, name="ident_bf")
+        make_identity(nc, ident_bf[:])
+        warm = keep.tile([P, 1], F32, name="warm")
+        nc.gpsimd.memset(warm[:], 1.0)
+        warm2 = keep.tile([P, 1], F32, name="warm2")
+        nc.scalar.activation(out=warm2[:], in_=warm[:], func=ACT.Sqrt)
+
+        tab_a = []
+        tab_b = []
+        for qk in range(2):
+            g4 = gains[qk][:].rearrange("p (j e) -> p j e", e=2).unsqueeze(1)
+            ta = keep.tile([P, 2, 64, 2], F32, name="tab_a_%d" % qk)
+            tb = keep.tile([P, 2, 64, 2], F32, name="tab_b_%d" % qk)
+            nc.vector.tensor_tensor(out=ta[:], in0=g4.to_broadcast([P, 2, 64, 2]), in1=fc[:, :, :, 0:1].to_broadcast([P, 2, 64, 2]), op=ALU.mult)
+            nc.vector.tensor_tensor(out=tb[:, :, :, 0:1], in0=g4[:, :, :, 0:1].to_broadcast([P, 2, 64, 1]), in1=fc[:, :, :, 1:2], op=ALU.mult)
+            nc.vector.scalar_tensor_tensor(
+                out=tb[:, :, :, 1:2], in0=g4[:, :, :, 1:2].to_broadcast([P, 2, 64, 1]), scalar=-1.0, in1=fc[:, :, :, 1:2],
+                op0=ALU.mult, op1=ALU.mult,
+            )
+            tab_a.append(ta)
+            tab_b.append(tb)
+
+        x_codes = keep.tile([P, PASSES, 512], U32, name="x_codes", align_bytes=64)
+        x_scales = keep.tile([P, PASSES, 512], U8, name="x_scales", align_bytes=64)
+
+        wide = {}
+        grouped = {}
+        w_codes = {}
+        w_scales = {}
+        acc = {}
+        rope = {}
+        sumsq = {}
+        rstd = {}
+        roots = {}
+        casts = {}
+
+        def widen(t):
+            wd = wide_pool.tile([P, D], BF16, name="wide_%d" % t, tag="wide")
+            pieces = 4 if t == 0 else 1
+            first = 512 * S_PASSES[t // 4] if t % 4 == 3 else 0
+            width = (D - first) // pieces
+            for c in range(pieces):
+                cols = slice(first + width * c, first + width * (c + 1))
+                nc.vector.tensor_tensor(out=wd[:, cols], in0=w_bytes[t][:, cols].bitcast(FP8), in1=scale_b[:, cols], op=ALU.mult)
+            wide[t] = wd
+
+        def cast(g):
+            cs = cast_pool.tile([P, 512 * S_PASSES[g]], BF16, name="cast_%d" % g, tag="cast")
+            nc.scalar.copy(out=cs[:], in_=w_bytes[4 * g + 3][:, 0 : 512 * S_PASSES[g]].bitcast(FP8))
+            casts[g] = cs
+
+        def unit_words(k, j):
+            if k < PASSES:
+                return x_raw[k][:, j, :].bitcast(F32)
+            g, p = divmod(k - PASSES, PASSES)
+            return wide[4 * g + j][:].bitcast(F32)[:, 256 * p : 256 * (p + 1)]
+
+        def turn(k):
+            gr = grouped_pool.tile([P, D], BF16, name="grouped_%d" % k, tag="grouped", align_bytes=64)
+            grouped[k] = gr
+            g, p = divmod(k - PASSES, PASSES)
+            by_scalar = k >= PASSES and p < S_PASSES[g]
+            banks = []
+            for pair in range(2):
+                tp = psum_t.tile([P, 512], F32, name="tp_%d_%d" % (k, pair), tag="tp")
+                banks.append(tp)
+                if pair == 1 and by_scalar:
+                    words = unit_words(k, 2)
+                    for u in range(2):
+                        nc.tensor.transpose(tp[:, P * u : P * (u + 1)], words[:, u : 256 : 2], ident[:])
+                    planes = tp[:, 256:512].bitcast(BF16)
+                    for t in range(4):
+                        nc.tensor.transpose(planes[:, P * t : P * (t + 1)], casts[g][:, 512 * p + t : 512 * (p + 1) : 4], ident_bf[:])
+                else:
+                    for jj in range(2):
+                        words = unit_words(k, 2 * pair + jj)
+                        for u in range(2):
+                            nc.tensor.transpose(tp[:, 256 * u + P * jj : 256 * u + P * (jj + 1)], words[:, u : 256 : 2], ident[:])
+            for pair in range(2):
+                if pair == 1 and by_scalar:
+                    nc.scalar.copy(
+                        out=gr[:, 1024:1536].bitcast(F32).rearrange("p (n u) -> p n u", u=2),
+                        in_=banks[1][:, 0:256].rearrange("p (u n) -> p n u", u=2),
+                    )
+                    planes = banks[1][:, 256:512].bitcast(BF16)
+                    for t in range(4):
+                        nc.scalar.activation(
+                            out=gr[:, 1536:2048].rearrange("p (n t) -> p n t", t=4)[:, :, t : t + 1],
+                            in_=planes[:, P * t : P * (t + 1)].unsqueeze(2),
+                            func=ACT.Copy,
+                            scale=scale_col[:, 4 * p + t : 4 * p + t + 1],
+                        )
+                else:
+                    nc.scalar.copy(
+                        out=gr[:, 1024 * pair : 1024 * (pair + 1)].bitcast(F32).rearrange("p (n u) -> p n u", u=2),
+                        in_=banks[pair][:].rearrange("p (u n) -> p n u", u=2),
+                    )
+
+        def quantize(k):
+            if k < PASSES:
+                codes, scales = x_codes[:, k, :], x_scales[:, k, :]
+            else:
+                g, p = divmod(k - PASSES, PASSES)
+                if p == 0:
+                    w_codes[g] = codes_pool.tile([P, PASSES, 512], U32, name="w_codes_%d" % g, tag="w_codes", align_bytes=64)
+                    w_scales[g] = codes_pool.tile([P, PASSES, 512], U8, name="w_scales_%d" % g, tag="w_scales", align_bytes=64)
+                codes, scales = w_codes[g][:, p, :], w_scales[g][:, p, :]
+            nc.vector.quantize_mx(out=codes.bitcast(FP8X4), scales=scales, in_=grouped[k][:])
+
+        def multiply(g, m):
+            if g < ROPE_GROUPS:
+                a = psum_acc.tile([P, 512], F32, name="acc_%d_%d" % (g, m), tag="acc")
+            else:
+                a = psum_t.tile([P, 512], F32, name="acc_%d_%d" % (g, m), tag="tp")
+            acc[(g, m)] = a
+            for p in range(PASSES):
+                nc.tensor.matmul_mx(
+                    out=a[:],
+                    lhsT=x_codes[:, p, P * m : P * (m + 1)].bitcast(FP8X4),
+                    lhsT_scale=x_scales[:, p, P * m : P * (m + 1)],
+                    rhs=w_codes[g][:, p, :].bitcast(FP8X4),
+                    rhs_scale=w_scales[g][:, p, :],
+                    start=(p == 0),
+                    stop=(p == PASSES - 1),
+                )
+
+        def store(g, m, tile_ap):
+            rows = slice(P * m, P * (m + 1))
+            if g < 4:
+                dst = outs[0][rows, 512 * g : 512 * (g + 1)]
+            else:
+                dst = outs[g - 3][rows, :]
+            nc.sync.dma_start(out=dst, in_=tile_ap)
+
+        def squares(g, m):
+            if m == 0:
+                sumsq[g] = stat_pool.tile([P, 16], F32, name="sumsq_%d" % g, tag="sumsq")
+            for h in range(4):
+                junk = stat_pool.tile([P, 128], F32, name="junk_%d_%d_%d" % (g, m, h), tag="junk")
+                nc.scalar.activation(
+                    out=junk[:], in_=acc[(g, m)][:, P * h : P * (h + 1)], func=ACT.Square,
+                    accum_out=sumsq[g][:, 4 * m + h : 4 * m + h + 1],
+                )
+
+        def root(g):
+            rt = stat_pool.tile([P, 16], F32, name="root_%d" % g, tag="root")
+            nc.scalar.activation(out=rt[:], in_=sumsq[g][:], func=ACT.Sqrt, scale=1.0 / 128.0, bias=EPS)
+            roots[g] = rt
+
+        def products(g, m):
+            qk = 0 if g < 4 else 1
+            st = m % 2
+            a3 = acc[(g, m)][:].rearrange("p (h c) -> p h c", h=4)
+            t1 = rope_pool.tile([P, 512], F32, name="t1_%d_%d" % (g, m), tag="t1")
+            t2 = rope_pool.tile([P, 512], F32, name="t2_%d_%d" % (g, m), tag="t2")
+            ta = tab_a[qk][:, st, :, :].rearrange("p j e -> p (j e)").unsqueeze(1).to_broadcast([P, 4, 128])
+            tb = tab_b[qk][:, st, :, :].rearrange("p j e -> p (j e)").unsqueeze(1).to_broadcast([P, 4, 128])
+            nc.vector.tensor_tensor(out=t1[:].rearrange("p (h c) -> p h c", h=4), in0=a3, in1=ta, op=ALU.mult)
+            nc.vector.tensor_tensor(out=t2[:].rearrange("p (h c) -> p h c", h=4), in0=a3, in1=tb, op=ALU.mult)
+            rope[(g, m)] = (t1, t2)
+
+        def combine(engine, g, m):
+            t1, t2 = rope[(g, m)]
+            engine.tensor_tensor(
+                out=t1[:].rearrange("p (n e) -> p n e", e=2),
+                in0=t1[:].rearrange("p (n e) -> p n e", e=2),
+                in1=t2[:].rearrange("p (n e) -> p n e", e=2)[:, :, ::-1],
+                op=ALU.add,
+            )
+
+        def burst(g):
+            for m in range(TOK_TILES):
+                products(g, m)
+                if m < 3:
+                    combine(nc.gpsimd, g, m)
+                if m == 2:
+                    rstd[g] = stat_pool.tile([P, 16], F32, name="rstd_%d" % g, tag="rstd")
+                    nc.vector.reciprocal(out=rstd[g][:], in_=roots[g][:])
+
+        def finish(g, m):
+            o = out_pool.tile([P, 512], F32, name="o_%d_%d" % (g, m), tag="o")
+            for h in range(4):
+                nc.scalar.activation(
+                    out=o[:, P * h : P * (h + 1)], in_=rope[(g, m)][0][:, P * h : P * (h + 1)], func=ACT.Copy,
+                    scale=rstd[g][:, 4 * m + h : 4 * m + h + 1],
+                )
+            store(g, m, o[:])
+
+        def finish_on_vector(g, m):
+            o = out_pool.tile([P, 512], F32, name="o_%d_%d" % (g, m), tag="o")
+            nc.vector.tensor_tensor(
+                out=o[:].rearrange("p (h c) -> p h c", h=4),
+                in0=rope[(g, m)][0][:].rearrange("p (h c) -> p h c", h=4),
+                in1=rstd[g][:, 4 * m : 4 * (m + 1)].unsqueeze(2).to_broadcast([P, 4, 128]),
+                op=ALU.mult,
+            )
+            store(g, m, o[:])
+
+        def plain_out(g, m):
+            o = out_pool.tile([P, 512], F32, name="o_%d_%d" % (g, m), tag="o")
+            nc.scalar.copy(out=o[:], in_=acc[(g, m)][:])
+            store(g, m, o[:])
+
+        def turn_tick(k):
+            if k < PASSES:
+                return k // 2
+            return k - 1 if k <= 24 else 23 + (k - 24) // 2
+
+        def quantize_tick(k):
+            return k + 1 if k <= 23 else 24 + (k - 24) // 2
+
+        def burst_tick(g):
+            return 4 * g + 11 if g < 4 else 25
+
+        def multiply_tick(g, m):
+            return 4 * g + 8 + m // 2 if g < 4 else 24
+
+        for tick in range(26):
+            if tick < ROW_TILES:
+                widen(tick)
+            for k in range(UNITS):
+                if turn_tick(k) == tick:
+                    turn(k)
+            for g in range(GROUPS):
+                if max(4 * g - 1, 0) == tick and S_PASSES[g] > 0:
+                    cast(g)
+            for g in range(4):
+                for m in range(TOK_TILES):
+                    if burst_tick(g) + 1 + m // 3 == tick:
+                        finish(g, m)
+            for k in range(UNITS):
+                if quantize_tick(k) == tick:
+                    quantize(k)
+            for g in range(4):
+                if burst_tick(g) + 1 == tick:
+                    combine(nc.vector, g, 3)
+            for g in range(ROPE_GROUPS):
+                for m in range(TOK_TILES):
+                    if multiply_tick(g, m) == tick:
+                        multiply(g, m)
+                        squares(g, m)
+                        if m == 3:
+                            root(g)
+            if tick == 25:
+                for m in range(TOK_TILES):
+                    multiply(5, m)
+            for g in range(ROPE_GROUPS):
+                if burst_tick(g) == tick:
+                    burst(g)
+            if tick == 25:
+                plain_out(5, 0)
+                finish(4, 0)
+                plain_out(5, 1)
+                finish(4, 1)
+                plain_out(5, 2)
+                plain_out(5, 3)
+                combine(nc.vector, 4, 3)
+                finish_on_vector(4, 2)
+                finish_on_vector(4, 3)

@@ -39,18 +39,27 @@ def tile_attention_pa_kernel(tc, x, freqs_cis, wqkv_bytes, wqkv_scale, q_norm_w,
     with ExitStack() as ctx:
         keep = ctx.enter_context(tc.tile_pool(name="keep", bufs=1))
         bytes_pool = ctx.enter_context(tc.tile_pool(name="bytes_pool", bufs=ROW_TILES))
-        wide_pool = ctx.enter_context(tc.tile_pool(name="wide_pool", bufs=10))
+        wide_pool = ctx.enter_context(tc.tile_pool(name="wide_pool", bufs=8))
         cast_pool = ctx.enter_context(tc.tile_pool(name="cast_pool", bufs=2))
-        grouped_pool = ctx.enter_context(tc.tile_pool(name="grouped_pool", bufs=5))
+        grouped_pool = ctx.enter_context(tc.tile_pool(name="grouped_pool", bufs=7))
         codes_pool = ctx.enter_context(tc.tile_pool(name="codes_pool", bufs=3))
         rope_pool = ctx.enter_context(tc.tile_pool(name="rope_pool", bufs=4))
-        out_pool = ctx.enter_context(tc.tile_pool(name="out_pool", bufs=6))
+        sum_pool = ctx.enter_context(tc.tile_pool(name="sum_pool", bufs=8))
+        out_pool = ctx.enter_context(tc.tile_pool(name="out_pool", bufs=10))
         stat_pool = ctx.enter_context(tc.tile_pool(name="stat_pool", bufs=2))
         psum_t = ctx.enter_context(tc.psum_pool(name="psum_t", bufs=4))
         psum_acc = ctx.enter_context(tc.psum_pool(name="psum_acc", bufs=4))
         if MANUAL:
             ctx.enter_context(tc.manual_schedule())
 
+        scale_b = keep.tile([P, D], F32, name="scale_b")
+        scale_row = wqkv_scale.rearrange("o k -> (o k)")
+
+        def load_scales(c):
+            nc.sync.dma_start(out=scale_b[:, 512 * c : 512 * (c + 1)], in_=scale_row[512 * c : 512 * (c + 1)].partition_broadcast(P))
+
+        scale_col = keep.tile([P, 16], F32, name="scale_col")
+        nc.scalar.dma_start(out=scale_col[:].rearrange("p (g t) -> p g t", t=4), in_=wqkv_scale.rearrange("o (g p t) -> p (o g) t", p=P, t=4))
         fc = keep.tile([P, 2, 64, 2], BF16, name="fc")
         nc.scalar.dma_start(out=fc[:].rearrange("p t j e -> p t (j e)"), in_=freqs_cis.rearrange("(t p) j e -> p t (j e)", p=P))
         gains = []
@@ -58,13 +67,6 @@ def tile_attention_pa_kernel(tc, x, freqs_cis, wqkv_bytes, wqkv_scale, q_norm_w,
             g_t = keep.tile([P, 128], BF16, name=name)
             nc.scalar.dma_start(out=g_t[:], in_=vec.partition_broadcast(P))
             gains.append(g_t)
-        scale_b = keep.tile([P, D], F32, name="scale_b")
-        scale_row = wqkv_scale.rearrange("o k -> (o k)")
-        for c in range(4):
-            nc.scalar.dma_start(out=scale_b[:, 512 * c : 512 * (c + 1)], in_=scale_row[512 * c : 512 * (c + 1)].partition_broadcast(P))
-
-        scale_col = keep.tile([P, 16], F32, name="scale_col")
-        nc.scalar.dma_start(out=scale_col[:].rearrange("p (g t) -> p g t", t=4), in_=wqkv_scale.rearrange("o (g p t) -> p (o g) t", p=P, t=4))
 
         w_bytes = []
         x_raw = []
@@ -79,14 +81,15 @@ def tile_attention_pa_kernel(tc, x, freqs_cis, wqkv_bytes, wqkv_scale, q_norm_w,
             nc.sync.dma_start(out=xr[:], in_=x_rows[:, :, 512 * c : 512 * (c + 1)])
             x_raw.append(xr)
 
+        load_scales(0)
         load_w(0)
-        load_x(0)
+        for c in range(1, PASSES):
+            load_scales(c)
         load_w(1)
-        load_x(1)
-        load_x(2)
-        load_w(2)
-        load_x(3)
-        for t in range(3, ROW_TILES):
+        for c in range(PASSES):
+            load_x(c)
+            load_w(2 + c)
+        for t in range(6, ROW_TILES):
             load_w(t)
 
         ident = keep.tile([P, P], F32, name="ident")
@@ -100,18 +103,20 @@ def tile_attention_pa_kernel(tc, x, freqs_cis, wqkv_bytes, wqkv_scale, q_norm_w,
 
         tab_a = []
         tab_b = []
-        for qk in range(2):
-            g4 = gains[qk][:].rearrange("p (j e) -> p j e", e=2).unsqueeze(1)
-            ta = keep.tile([P, 2, 64, 2], F32, name="tab_a_%d" % qk)
-            tb = keep.tile([P, 2, 64, 2], F32, name="tab_b_%d" % qk)
-            nc.vector.tensor_tensor(out=ta[:], in0=g4.to_broadcast([P, 2, 64, 2]), in1=fc[:, :, :, 0:1].to_broadcast([P, 2, 64, 2]), op=ALU.mult)
-            nc.vector.tensor_tensor(out=tb[:, :, :, 0:1], in0=g4[:, :, :, 0:1].to_broadcast([P, 2, 64, 1]), in1=fc[:, :, :, 1:2], op=ALU.mult)
-            nc.vector.scalar_tensor_tensor(
-                out=tb[:, :, :, 1:2], in0=g4[:, :, :, 1:2].to_broadcast([P, 2, 64, 1]), scalar=-1.0, in1=fc[:, :, :, 1:2],
-                op0=ALU.mult, op1=ALU.mult,
-            )
-            tab_a.append(ta)
-            tab_b.append(tb)
+
+        def tables():
+            for qk in range(2):
+                g4 = gains[qk][:].rearrange("p (j e) -> p j e", e=2).unsqueeze(1)
+                ta = keep.tile([P, 2, 64, 2], F32, name="tab_a_%d" % qk)
+                tb = keep.tile([P, 2, 64, 2], F32, name="tab_b_%d" % qk)
+                nc.vector.tensor_tensor(out=ta[:], in0=g4.to_broadcast([P, 2, 64, 2]), in1=fc[:, :, :, 0:1].to_broadcast([P, 2, 64, 2]), op=ALU.mult)
+                nc.vector.tensor_tensor(out=tb[:, :, :, 0:1], in0=g4[:, :, :, 0:1].to_broadcast([P, 2, 64, 1]), in1=fc[:, :, :, 1:2], op=ALU.mult)
+                nc.vector.scalar_tensor_tensor(
+                    out=tb[:, :, :, 1:2], in0=g4[:, :, :, 1:2].to_broadcast([P, 2, 64, 1]), scalar=-1.0, in1=fc[:, :, :, 1:2],
+                    op0=ALU.mult, op1=ALU.mult,
+                )
+                tab_a.append(ta)
+                tab_b.append(tb)
 
         x_codes = keep.tile([P, PASSES, 512], U32, name="x_codes", align_bytes=64)
         x_scales = keep.tile([P, PASSES, 512], U8, name="x_scales", align_bytes=64)
@@ -136,6 +141,13 @@ def tile_attention_pa_kernel(tc, x, freqs_cis, wqkv_bytes, wqkv_scale, q_norm_w,
                 cols = slice(first + width * c, first + width * (c + 1))
                 nc.vector.tensor_tensor(out=wd[:, cols], in0=w_bytes[t][:, cols].bitcast(FP8), in1=scale_b[:, cols], op=ALU.mult)
             wide[t] = wd
+
+        def widen_last(c):
+            cols = slice(512 * c, 512 * (c + 1))
+            for t in range(20, ROW_TILES):
+                if c == 0:
+                    wide[t] = wide_pool.tile([P, D], BF16, name="wide_%d" % t, tag="wide")
+                nc.vector.tensor_tensor(out=wide[t][:, cols], in0=w_bytes[t][:, cols].bitcast(FP8), in1=scale_b[:, cols], op=ALU.mult)
 
         def cast(g):
             cs = cast_pool.tile([P, 512 * S_PASSES[g]], BF16, name="cast_%d" % g, tag="cast")
@@ -244,7 +256,7 @@ def tile_attention_pa_kernel(tc, x, freqs_cis, wqkv_bytes, wqkv_scale, q_norm_w,
             qk = 0 if g < 4 else 1
             st = m % 2
             a3 = acc[(g, m)][:].rearrange("p (h c) -> p h c", h=4)
-            t1 = rope_pool.tile([P, 512], F32, name="t1_%d_%d" % (g, m), tag="t1")
+            t1 = sum_pool.tile([P, 512], F32, name="t1_%d_%d" % (g, m), tag="t1")
             t2 = rope_pool.tile([P, 512], F32, name="t2_%d_%d" % (g, m), tag="t2")
             ta = tab_a[qk][:, st, :, :].rearrange("p j e -> p (j e)").unsqueeze(1).to_broadcast([P, 4, 128])
             tb = tab_b[qk][:, st, :, :].rearrange("p j e -> p (j e)").unsqueeze(1).to_broadcast([P, 4, 128])
@@ -261,14 +273,19 @@ def tile_attention_pa_kernel(tc, x, freqs_cis, wqkv_bytes, wqkv_scale, q_norm_w,
                 op=ALU.add,
             )
 
-        def burst(g):
+        def burst(g, follow):
+            if g == 4:
+                rstd[g] = stat_pool.tile([P, 16], F32, name="rstd_%d" % g, tag="rstd")
+                nc.vector.reciprocal(out=rstd[g][:], in_=roots[g][:])
             for m in range(TOK_TILES):
                 products(g, m)
                 if m < 3:
                     combine(nc.gpsimd, g, m)
-                if m == 2:
+                if m == 2 and g < 4:
                     rstd[g] = stat_pool.tile([P, 16], F32, name="rstd_%d" % g, tag="rstd")
                     nc.vector.reciprocal(out=rstd[g][:], in_=roots[g][:])
+                if follow is not None:
+                    follow(m)
 
         def finish(g, m):
             o = out_pool.tile([P, 512], F32, name="o_%d_%d" % (g, m), tag="o")
@@ -296,26 +313,42 @@ def tile_attention_pa_kernel(tc, x, freqs_cis, wqkv_bytes, wqkv_scale, q_norm_w,
 
         def turn_tick(k):
             if k < PASSES:
-                return k // 2
-            return k - 1 if k <= 24 else 23 + (k - 24) // 2
+                return k + 1
+            if k <= 23:
+                return k - 1
+            return (21, 22, 23, 23)[k - 24]
 
         def quantize_tick(k):
-            return k + 1 if k <= 23 else 24 + (k - 24) // 2
+            if k < PASSES:
+                return k + 3
+            if k <= 22:
+                return k + 1
+            return 23 if k == 23 else 24
 
         def burst_tick(g):
             return 4 * g + 11 if g < 4 else 25
 
         def multiply_tick(g, m):
-            return 4 * g + 8 + m // 2 if g < 4 else 24
+            return 4 * g + 8 + m // 2
+
+        def next_group(m):
+            multiply(4, m)
+            squares(4, m)
+            if m == 3:
+                root(4)
 
         for tick in range(26):
-            if tick < ROW_TILES:
+            if tick < 20:
                 widen(tick)
+            elif tick < ROW_TILES:
+                widen_last(tick - 20)
+            if tick == 5:
+                tables()
             for k in range(UNITS):
                 if turn_tick(k) == tick:
                     turn(k)
             for g in range(GROUPS):
-                if max(4 * g - 1, 0) == tick and S_PASSES[g] > 0:
+                if max(4 * g - 1, 2) == tick and S_PASSES[g] > 0:
                     cast(g)
             for g in range(4):
                 for m in range(TOK_TILES):
@@ -327,19 +360,19 @@ def tile_attention_pa_kernel(tc, x, freqs_cis, wqkv_bytes, wqkv_scale, q_norm_w,
             for g in range(4):
                 if burst_tick(g) + 1 == tick:
                     combine(nc.vector, g, 3)
-            for g in range(ROPE_GROUPS):
+            for g in range(4):
                 for m in range(TOK_TILES):
                     if multiply_tick(g, m) == tick:
                         multiply(g, m)
                         squares(g, m)
                         if m == 3:
                             root(g)
-            if tick == 25:
+            if tick == 24:
                 for m in range(TOK_TILES):
                     multiply(5, m)
             for g in range(ROPE_GROUPS):
                 if burst_tick(g) == tick:
-                    burst(g)
+                    burst(g, next_group if g == 3 else None)
             if tick == 25:
                 plain_out(5, 0)
                 finish(4, 0)

@@ -54,9 +54,8 @@ def tile_attention_pa_kernel(tc, x, freqs_cis, wqkv_bytes, wqkv_scale, q_norm_w,
 
         scale_b = keep.tile([P, D], F32, name="scale_b")
         scale_row = wqkv_scale.rearrange("o k -> (o k)")
-
-        def load_scales(c):
-            nc.sync.dma_start(out=scale_b[:, 512 * c : 512 * (c + 1)], in_=scale_row[512 * c : 512 * (c + 1)].partition_broadcast(P))
+        for c in range(4):
+            nc.scalar.dma_start(out=scale_b[:, 512 * c : 512 * (c + 1)], in_=scale_row[512 * c : 512 * (c + 1)].partition_broadcast(P))
 
         scale_col = keep.tile([P, 16], F32, name="scale_col")
         nc.scalar.dma_start(out=scale_col[:].rearrange("p (g t) -> p g t", t=4), in_=wqkv_scale.rearrange("o (g p t) -> p (o g) t", p=P, t=4))
@@ -81,10 +80,7 @@ def tile_attention_pa_kernel(tc, x, freqs_cis, wqkv_bytes, wqkv_scale, q_norm_w,
             nc.sync.dma_start(out=xr[:], in_=x_rows[:, :, 512 * c : 512 * (c + 1)])
             x_raw.append(xr)
 
-        load_scales(0)
         load_w(0)
-        for c in range(1, PASSES):
-            load_scales(c)
         load_w(1)
         for c in range(PASSES):
             load_x(c)

@@ -52,13 +52,6 @@ def tile_attention_pa_kernel(tc, x, freqs_cis, wqkv_bytes, wqkv_scale, q_norm_w,
         if MANUAL:
             ctx.enter_context(tc.manual_schedule())
 
-        scale_b = keep.tile([P, D], F32, name="scale_b")
-        scale_row = wqkv_scale.rearrange("o k -> (o k)")
-        for c in range(4):
-            nc.scalar.dma_start(out=scale_b[:, 512 * c : 512 * (c + 1)], in_=scale_row[512 * c : 512 * (c + 1)].partition_broadcast(P))
-
-        scale_col = keep.tile([P, 16], F32, name="scale_col")
-        nc.scalar.dma_start(out=scale_col[:].rearrange("p (g t) -> p g t", t=4), in_=wqkv_scale.rearrange("o (g p t) -> p (o g) t", p=P, t=4))
         fc = keep.tile([P, 2, 64, 2], BF16, name="fc")
         nc.scalar.dma_start(out=fc[:].rearrange("p t j e -> p t (j e)"), in_=freqs_cis.rearrange("(t p) j e -> p t (j e)", p=P))
         gains = []
@@ -66,6 +59,13 @@ def tile_attention_pa_kernel(tc, x, freqs_cis, wqkv_bytes, wqkv_scale, q_norm_w,
             g_t = keep.tile([P, 128], BF16, name=name)
             nc.scalar.dma_start(out=g_t[:], in_=vec.partition_broadcast(P))
             gains.append(g_t)
+        scale_b = keep.tile([P, D], F32, name="scale_b")
+        scale_row = wqkv_scale.rearrange("o k -> (o k)")
+        for c in range(4):
+            nc.scalar.dma_start(out=scale_b[:, 512 * c : 512 * (c + 1)], in_=scale_row[512 * c : 512 * (c + 1)].partition_broadcast(P))
+
+        scale_col = keep.tile([P, 16], F32, name="scale_col")
+        nc.scalar.dma_start(out=scale_col[:].rearrange("p (g t) -> p g t", t=4), in_=wqkv_scale.rearrange("o (g p t) -> p (o g) t", p=P, t=4))
 
         w_bytes = []
         x_raw = []
@@ -113,6 +113,8 @@ def tile_attention_pa_kernel(tc, x, freqs_cis, wqkv_bytes, wqkv_scale, q_norm_w,
                 )
                 tab_a.append(ta)
                 tab_b.append(tb)
+
+        tables()
 
         x_codes = keep.tile([P, PASSES, 512], U32, name="x_codes", align_bytes=64)
         x_scales = keep.tile([P, PASSES, 512], U8, name="x_scales", align_bytes=64)
@@ -338,8 +340,6 @@ def tile_attention_pa_kernel(tc, x, freqs_cis, wqkv_bytes, wqkv_scale, q_norm_w,
                 widen(tick)
             elif tick < ROW_TILES:
                 widen_last(tick - 20)
-            if tick == 5:
-                tables()
             for k in range(UNITS):
                 if turn_tick(k) == tick:
                     turn(k)

@@ -52,20 +52,15 @@ def tile_attention_pa_kernel(tc, x, freqs_cis, wqkv_bytes, wqkv_scale, q_norm_w,
         if MANUAL:
             ctx.enter_context(tc.manual_schedule())
 
-        fc = keep.tile([P, 2, 64, 2], BF16, name="fc")
-        nc.scalar.dma_start(out=fc[:].rearrange("p t j e -> p t (j e)"), in_=freqs_cis.rearrange("(t p) j e -> p t (j e)", p=P))
-        gains = []
-        for name, vec in (("gain_q", q_norm_w), ("gain_k", k_norm_w)):
-            g_t = keep.tile([P, 128], BF16, name=name)
-            nc.scalar.dma_start(out=g_t[:], in_=vec.partition_broadcast(P))
-            gains.append(g_t)
-        scale_b = keep.tile([P, D], F32, name="scale_b")
-        scale_row = wqkv_scale.rearrange("o k -> (o k)")
-        for c in range(4):
-            nc.scalar.dma_start(out=scale_b[:, 512 * c : 512 * (c + 1)], in_=scale_row[512 * c : 512 * (c + 1)].partition_broadcast(P))
-
         scale_col = keep.tile([P, 16], F32, name="scale_col")
         nc.scalar.dma_start(out=scale_col[:].rearrange("p (g t) -> p g t", t=4), in_=wqkv_scale.rearrange("o (g p t) -> p (o g) t", p=P, t=4))
+        gain_col = []
+        for name, vec in (("gain_col_q", q_norm_w), ("gain_col_k", k_norm_w)):
+            g_c = keep.tile([P, 1], BF16, name=name)
+            nc.scalar.dma_start(out=g_c[:], in_=vec.rearrange("(p o) -> p o", o=1))
+            gain_col.append(g_c)
+        fc = keep.tile([P, 2, 64, 2], BF16, name="fc")
+        nc.scalar.dma_start(out=fc[:].rearrange("p t j e -> p t (j e)"), in_=freqs_cis.rearrange("(t p) j e -> p t (j e)", p=P))
 
         w_bytes = []
         x_raw = []
@@ -88,14 +83,31 @@ def tile_attention_pa_kernel(tc, x, freqs_cis, wqkv_bytes, wqkv_scale, q_norm_w,
         for t in range(6, ROW_TILES):
             load_w(t)
 
-        ident = keep.tile([P, P], F32, name="ident")
-        make_identity(nc, ident[:])
-        ident_bf = keep.tile([P, P], BF16, name="ident_bf")
-        make_identity(nc, ident_bf[:])
         warm = keep.tile([P, 1], F32, name="warm")
         nc.gpsimd.memset(warm[:], 1.0)
         warm2 = keep.tile([P, 1], F32, name="warm2")
         nc.scalar.activation(out=warm2[:], in_=warm[:], func=ACT.Sqrt)
+        ident_bf = keep.tile([P, P], BF16, name="ident_bf")
+        make_identity(nc, ident_bf[:])
+        ident = keep.tile([P, P], F32, name="ident")
+        make_identity(nc, ident[:])
+
+        gains_ps = psum_t.tile([P, 512], F32, name="gains_ps", tag="tp")
+        gains = []
+        for qk, name in enumerate(("gain_q", "gain_k")):
+            nc.tensor.transpose(gains_ps[:].bitcast(BF16)[:, P * qk : P * (qk + 1)], gain_col[qk][:].to_broadcast([P, P]), ident_bf[:])
+            g_t = keep.tile([P, 128], BF16, name=name)
+            nc.scalar.copy(out=g_t[:], in_=gains_ps[:].bitcast(BF16)[:, P * qk : P * (qk + 1)])
+            gains.append(g_t)
+        scale_b = keep.tile([P, D], F32, name="scale_b")
+        for g in range(PASSES):
+            sp = psum_t.tile([P, 512], F32, name="scale_ps_%d" % g, tag="tp")
+            for t in range(4):
+                nc.tensor.transpose(sp[:, P * t : P * (t + 1)], scale_col[:, 4 * g + t : 4 * g + t + 1].to_broadcast([P, P]), ident[:])
+            nc.scalar.copy(
+                out=scale_b[:, 512 * g : 512 * (g + 1)].rearrange("p (n t) -> p n t", t=4),
+                in_=sp[:].rearrange("p (t n) -> p n t", t=4),
+            )
 
         tab_a = []
         tab_b = []

@@ -46,7 +46,7 @@ def tile_attention_pa_kernel(tc, x, freqs_cis, wqkv_bytes, wqkv_scale, q_norm_w,
         rope_pool = ctx.enter_context(tc.tile_pool(name="rope_pool", bufs=4))
         sum_pool = ctx.enter_context(tc.tile_pool(name="sum_pool", bufs=8))
         out_pool = ctx.enter_context(tc.tile_pool(name="out_pool", bufs=10))
-        stat_pool = ctx.enter_context(tc.tile_pool(name="stat_pool", bufs=2))
+        stat_pool = ctx.enter_context(tc.tile_pool(name="stat_pool", bufs=3))
         psum_t = ctx.enter_context(tc.psum_pool(name="psum_t", bufs=4))
         psum_acc = ctx.enter_context(tc.psum_pool(name="psum_acc", bufs=4))
         if MANUAL:
@@ -287,6 +287,14 @@ def tile_attention_pa_kernel(tc, x, freqs_cis, wqkv_bytes, wqkv_scale, q_norm_w,
             if g == 4:
                 rstd[g] = stat_pool.tile([P, 16], F32, name="rstd_%d" % g, tag="rstd")
                 nc.vector.reciprocal(out=rstd[g][:], in_=roots[g][:])
+            if g > 0:
+                if g == 4:
+                    gate_f = stat_pool.tile([P, 1], F32, name="gate_f", tag="gate_f")
+                    nc.gpsimd.tensor_copy(out=gate_f[:], in_=rstd[g][:, 0:1])
+                else:
+                    gate_u = stat_pool.tile([P, 1], U32, name="gate_u_%d" % g, tag="gate_u")
+                    nc.gpsimd.tensor_copy(out=gate_u[:], in_=w_codes[g + 1][:, 3 if g == 3 else 2, 0:1])
+                combine(nc.gpsimd, g - 1, 3)
             for m in range(TOK_TILES):
                 products(g, m)
                 if m < 3:
@@ -338,6 +346,9 @@ def tile_attention_pa_kernel(tc, x, freqs_cis, wqkv_bytes, wqkv_scale, q_norm_w,
         def burst_tick(g):
             return 4 * g + 11 if g < 4 else 25
 
+        def finish_tick(g, m):
+            return burst_tick(g) + 1 if m < 3 else burst_tick(g + 1) + 1
+
         def multiply_tick(g, m):
             return 4 * g + 8 + m // 2
 
@@ -360,14 +371,11 @@ def tile_attention_pa_kernel(tc, x, freqs_cis, wqkv_bytes, wqkv_scale, q_norm_w,
                     cast(g)
             for g in range(4):
                 for m in range(TOK_TILES):
-                    if burst_tick(g) + 1 + m // 3 == tick:
+                    if finish_tick(g, m) == tick:
                         finish(g, m)
             for k in range(UNITS):
                 if quantize_tick(k) == tick:
                     quantize(k)
-            for g in range(4):
-                if burst_tick(g) + 1 == tick:
-                    combine(nc.vector, g, 3)
             for g in range(4):
                 for m in range(TOK_TILES):
                     if multiply_tick(g, m) == tick:
@@ -382,6 +390,7 @@ def tile_attention_pa_kernel(tc, x, freqs_cis, wqkv_bytes, wqkv_scale, q_norm_w,
                 if burst_tick(g) == tick:
                     burst(g, next_group if g == 3 else None)
             if tick == 25:
+                finish(3, 3)
                 plain_out(5, 0)
                 finish(4, 0)
                 plain_out(5, 1)

@@ -288,22 +288,21 @@ def tile_attention_pa_kernel(tc, x, freqs_cis, wqkv_bytes, wqkv_scale, q_norm_w,
                 rstd[g] = stat_pool.tile([P, 16], F32, name="rstd_%d" % g, tag="rstd")
                 nc.vector.reciprocal(out=rstd[g][:], in_=roots[g][:])
             if g > 0:
-                if g == 4:
-                    gate_f = stat_pool.tile([P, 1], F32, name="gate_f", tag="gate_f")
-                    nc.gpsimd.tensor_copy(out=gate_f[:], in_=rstd[g][:, 0:1])
+                if g < 3:
+                    nc.gpsimd.memset(w_bytes[4 * g + 11][:, D - 1 : D], 0)
                 else:
-                    gate_u = stat_pool.tile([P, 1], U32, name="gate_u_%d" % g, tag="gate_u")
-                    nc.gpsimd.tensor_copy(out=gate_u[:], in_=w_codes[g + 1][:, 3 if g == 3 else 2, 0:1])
+                    nc.gpsimd.memset(grouped[22 if g == 3 else 26][:, 0:1], 0.0)
                 combine(nc.gpsimd, g - 1, 3)
             for m in range(TOK_TILES):
                 products(g, m)
-                if m < 3:
+                if m < 2:
                     combine(nc.gpsimd, g, m)
                 if m == 2 and g < 4:
                     rstd[g] = stat_pool.tile([P, 16], F32, name="rstd_%d" % g, tag="rstd")
                     nc.vector.reciprocal(out=rstd[g][:], in_=roots[g][:])
                 if follow is not None:
                     follow(m)
+            combine(nc.vector, g, 2)
 
         def finish(g, m):
             o = out_pool.tile([P, 512], F32, name="o_%d_%d" % (g, m), tag="o")

@@ -141,6 +141,7 @@ def tile_attention_pa_kernel(tc, x, freqs_cis, wqkv_bytes, wqkv_scale, q_norm_w,
         rstd = {}
         roots = {}
         casts = {}
+        sums = {}
 
         def widen(t):
             wd = wide_pool.tile([P, D], BF16, name="wide_%d" % t, tag="wide")
@@ -283,6 +284,16 @@ def tile_attention_pa_kernel(tc, x, freqs_cis, wqkv_bytes, wqkv_scale, q_norm_w,
                 op=ALU.add,
             )
 
+        def add_on_tensor(g, m):
+            t1, t2 = rope[(g, m)]
+            ps = psum_acc.tile([P, 512], F32, name="sum_%d_%d" % (g, m), tag="acc")
+            nc.tensor.matmul(out=ps[:], lhsT=ident[:], rhs=t1[:], start=True, stop=False)
+            nc.tensor.matmul(
+                out=ps[:].rearrange("p (n e) -> p n e", e=2), lhsT=ident[:],
+                rhs=t2[:].rearrange("p (n e) -> p n e", e=2)[:, :, ::-1], start=False, stop=True,
+            )
+            sums[(g, m)] = ps
+
         def burst(g, follow):
             if g == 4:
                 rstd[g] = stat_pool.tile([P, 16], F32, name="rstd_%d" % g, tag="rstd")
@@ -302,13 +313,14 @@ def tile_attention_pa_kernel(tc, x, freqs_cis, wqkv_bytes, wqkv_scale, q_norm_w,
                     nc.vector.reciprocal(out=rstd[g][:], in_=roots[g][:])
                 if follow is not None:
                     follow(m)
-            combine(nc.vector, g, 2)
+            if g >= 3:
+                combine(nc.vector, g, 2)
 
         def finish(g, m):
             o = out_pool.tile([P, 512], F32, name="o_%d_%d" % (g, m), tag="o")
             for h in range(4):
                 nc.scalar.activation(
-                    out=o[:, P * h : P * (h + 1)], in_=rope[(g, m)][0][:, P * h : P * (h + 1)], func=ACT.Copy,
+                    out=o[:, P * h : P * (h + 1)], in_=sums.get((g, m), rope[(g, m)][0])[:, P * h : P * (h + 1)], func=ACT.Copy,
                     scale=rstd[g][:, 4 * m + h : 4 * m + h + 1],
                 )
             store(g, m, o[:])
@@ -365,6 +377,9 @@ def tile_attention_pa_kernel(tc, x, freqs_cis, wqkv_bytes, wqkv_scale, q_norm_w,
             for k in range(UNITS):
                 if turn_tick(k) == tick:
                     turn(k)
+            for g in range(3):
+                if burst_tick(g) + 1 == tick:
+                    add_on_tensor(g, 2)
             for g in range(GROUPS):
                 if max(4 * g - 1, 2) == tick and S_PASSES[g] > 0:
                     cast(g)

@@ -24,7 +24,7 @@ ROPE_GROUPS = 5
 UNITS = 4 + 4 * GROUPS
 EPS = 1e-6
 MANUAL = True
-S_PASSES = (2, 3, 2, 2, 2, 0)
+V_PASSES = ((2, 4), (2, 3), (2, 3), (2, 3), (2, 4), (0, 4))
 
 
 def tile_attention_pa_kernel(tc, x, freqs_cis, wqkv_bytes, wqkv_scale, q_norm_w, k_norm_w, out_0, out_1, out_2):
@@ -99,6 +99,9 @@ def tile_attention_pa_kernel(tc, x, freqs_cis, wqkv_bytes, wqkv_scale, q_norm_w,
             g_t = keep.tile([P, 128], BF16, name=name)
             nc.scalar.copy(out=g_t[:], in_=gains_ps[:].bitcast(BF16)[:, P * qk : P * (qk + 1)])
             gains.append(g_t)
+        fi_signed = keep.tile([P, 2, 2, 64], BF16, name="fi_signed")
+        nc.scalar.copy(out=fi_signed[:, 0, :, :].unsqueeze(3), in_=fc[:, :, :, 1:2])
+        nc.scalar.activation(out=fi_signed[:, 1, :, :].unsqueeze(3), in_=fc[:, :, :, 1:2], func=ACT.Copy, scale=-1.0)
         scale_b = keep.tile([P, D], F32, name="scale_b")
         for g in range(PASSES):
             sp = psum_t.tile([P, 512], F32, name="scale_ps_%d" % g, tag="tp")
@@ -113,17 +116,16 @@ def tile_attention_pa_kernel(tc, x, freqs_cis, wqkv_bytes, wqkv_scale, q_norm_w,
         tab_b = []
 
         def tables():
+            g4 = []
             for qk in range(2):
-                g4 = gains[qk][:].rearrange("p (j e) -> p j e", e=2).unsqueeze(1)
+                g4.append(gains[qk][:].rearrange("p (j e) -> p j e", e=2).unsqueeze(1).to_broadcast([P, 2, 64, 2]))
+            for qk in range(2):
                 ta = keep.tile([P, 2, 64, 2], F32, name="tab_a_%d" % qk)
-                tb = keep.tile([P, 2, 64, 2], F32, name="tab_b_%d" % qk)
-                nc.vector.tensor_tensor(out=ta[:], in0=g4.to_broadcast([P, 2, 64, 2]), in1=fc[:, :, :, 0:1].to_broadcast([P, 2, 64, 2]), op=ALU.mult)
-                nc.vector.tensor_tensor(out=tb[:, :, :, 0:1], in0=g4[:, :, :, 0:1].to_broadcast([P, 2, 64, 1]), in1=fc[:, :, :, 1:2], op=ALU.mult)
-                nc.vector.scalar_tensor_tensor(
-                    out=tb[:, :, :, 1:2], in0=g4[:, :, :, 1:2].to_broadcast([P, 2, 64, 1]), scalar=-1.0, in1=fc[:, :, :, 1:2],
-                    op0=ALU.mult, op1=ALU.mult,
-                )
+                nc.vector.tensor_tensor(out=ta[:], in0=g4[qk], in1=fc[:, :, :, 0:1].to_broadcast([P, 2, 64, 2]), op=ALU.mult)
                 tab_a.append(ta)
+            for qk in range(2):
+                tb = keep.tile([P, 2, 64, 2], F32, name="tab_b_%d" % qk)
+                nc.vector.tensor_tensor(out=tb[:], in0=g4[qk], in1=fi_signed[:].rearrange("p e t j -> p t j e"), op=ALU.mult)
                 tab_b.append(tb)
 
         tables()
@@ -146,9 +148,9 @@ def tile_attention_pa_kernel(tc, x, freqs_cis, wqkv_bytes, wqkv_scale, q_norm_w,
         def widen(t):
             wd = wide_pool.tile([P, D], BF16, name="wide_%d" % t, tag="wide")
             pieces = 4 if t == 0 else 1
-            first = 512 * S_PASSES[t // 4] if t % 4 == 3 else 0
-            width = (D - first) // pieces
-            for c in range(pieces):
+            first, last = (512 * V_PASSES[t // 4][0], 512 * V_PASSES[t // 4][1]) if t % 4 == 3 else (0, D)
+            width = (last - first) // pieces
+            for c in range(pieces if last > first else 0):
                 cols = slice(first + width * c, first + width * (c + 1))
                 nc.vector.tensor_tensor(out=wd[:, cols], in0=w_bytes[t][:, cols].bitcast(FP8), in1=scale_b[:, cols], op=ALU.mult)
             wide[t] = wd
@@ -161,8 +163,10 @@ def tile_attention_pa_kernel(tc, x, freqs_cis, wqkv_bytes, wqkv_scale, q_norm_w,
                 nc.vector.tensor_tensor(out=wide[t][:, cols], in0=w_bytes[t][:, cols].bitcast(FP8), in1=scale_b[:, cols], op=ALU.mult)
 
         def cast(g):
-            cs = cast_pool.tile([P, 512 * S_PASSES[g]], BF16, name="cast_%d" % g, tag="cast")
-            nc.scalar.copy(out=cs[:], in_=w_bytes[4 * g + 3][:, 0 : 512 * S_PASSES[g]].bitcast(FP8))
+            cs = cast_pool.tile([P, D], BF16, name="cast_%d" % g, tag="cast")
+            for a, b in ((0, 512 * V_PASSES[g][0]), (512 * V_PASSES[g][1], D)):
+                if b > a:
+                    nc.scalar.copy(out=cs[:, a:b], in_=w_bytes[4 * g + 3][:, a:b].bitcast(FP8))
             casts[g] = cs
 
         def unit_words(k, j):
@@ -175,7 +179,7 @@ def tile_attention_pa_kernel(tc, x, freqs_cis, wqkv_bytes, wqkv_scale, q_norm_w,
             gr = grouped_pool.tile([P, D], BF16, name="grouped_%d" % k, tag="grouped", align_bytes=64)
             grouped[k] = gr
             g, p = divmod(k - PASSES, PASSES)
-            by_scalar = k >= PASSES and p < S_PASSES[g]
+            by_scalar = k >= PASSES and not V_PASSES[g][0] <= p < V_PASSES[g][1]
             banks = []
             for pair in range(2):
                 tp = psum_t.tile([P, 512], F32, name="tp_%d_%d" % (k, pair), tag="tp")
@@ -300,7 +304,8 @@ def tile_attention_pa_kernel(tc, x, freqs_cis, wqkv_bytes, wqkv_scale, q_norm_w,
                 nc.vector.reciprocal(out=rstd[g][:], in_=roots[g][:])
             if g > 0:
                 if g < 3:
-                    nc.gpsimd.memset(w_bytes[4 * g + 11][:, D - 1 : D], 0)
+                    gate_col = 512 * V_PASSES[g + 2][1] - 1
+                    nc.gpsimd.memset(w_bytes[4 * g + 11][:, gate_col : gate_col + 1], 0)
                 else:
                     nc.gpsimd.memset(grouped[22 if g == 3 else 26][:, 0:1], 0.0)
                 combine(nc.gpsimd, g - 1, 3)
@@ -381,7 +386,7 @@ def tile_attention_pa_kernel(tc, x, freqs_cis, wqkv_bytes, wqkv_scale, q_norm_w,
                 if burst_tick(g) + 1 == tick:
                     add_on_tensor(g, 2)
             for g in range(GROUPS):
-                if max(4 * g - 1, 2) == tick and S_PASSES[g] > 0:
+                if max(4 * g - 1, 2) == tick and V_PASSES[g][1] - V_PASSES[g][0] < PASSES:
                     cast(g)
             for g in range(4):
                 for m in range(TOK_TILES):

@@ -43,7 +43,6 @@ def tile_attention_pa_kernel(tc, x, freqs_cis, wqkv_bytes, wqkv_scale, q_norm_w,
         cast_pool = ctx.enter_context(tc.tile_pool(name="cast_pool", bufs=2))
         grouped_pool = ctx.enter_context(tc.tile_pool(name="grouped_pool", bufs=7))
         codes_pool = ctx.enter_context(tc.tile_pool(name="codes_pool", bufs=3))
-        rope_pool = ctx.enter_context(tc.tile_pool(name="rope_pool", bufs=4))
         sum_pool = ctx.enter_context(tc.tile_pool(name="sum_pool", bufs=8))
         out_pool = ctx.enter_context(tc.tile_pool(name="out_pool", bufs=10))
         stat_pool = ctx.enter_context(tc.tile_pool(name="stat_pool", bufs=3))
@@ -53,14 +52,14 @@ def tile_attention_pa_kernel(tc, x, freqs_cis, wqkv_bytes, wqkv_scale, q_norm_w,
             ctx.enter_context(tc.manual_schedule())
 
         scale_col = keep.tile([P, 16], F32, name="scale_col")
-        nc.scalar.dma_start(out=scale_col[:].rearrange("p (g t) -> p g t", t=4), in_=wqkv_scale.rearrange("o (g p t) -> p (o g) t", p=P, t=4))
+        nc.sync.dma_start(out=scale_col[:].rearrange("p (g t) -> p g t", t=4), in_=wqkv_scale.rearrange("o (g p t) -> p (o g) t", p=P, t=4))
+        fc = keep.tile([P, 2, 64, 2], BF16, name="fc")
+        nc.sync.dma_start(out=fc[:].rearrange("p t j e -> p t (j e)"), in_=freqs_cis.rearrange("(t p) j e -> p t (j e)", p=P))
         gain_col = []
         for name, vec in (("gain_col_q", q_norm_w), ("gain_col_k", k_norm_w)):
             g_c = keep.tile([P, 1], BF16, name=name)
             nc.scalar.dma_start(out=g_c[:], in_=vec.rearrange("(p o) -> p o", o=1))
             gain_col.append(g_c)
-        fc = keep.tile([P, 2, 64, 2], BF16, name="fc")
-        nc.scalar.dma_start(out=fc[:].rearrange("p t j e -> p t (j e)"), in_=freqs_cis.rearrange("(t p) j e -> p t (j e)", p=P))
 
         w_bytes = []
         x_raw = []
@@ -71,7 +70,7 @@ def tile_attention_pa_kernel(tc, x, freqs_cis, wqkv_bytes, wqkv_scale, q_norm_w,
             w_bytes.append(wb)
 
         def load_x(c):
-            xr = keep.tile([P, TOK_TILES, 512], BF16, name="x_raw_%d" % c)
+            xr = wide_pool.tile([P, TOK_TILES, 512], BF16, name="x_raw_%d" % c, tag="wide")
             nc.sync.dma_start(out=xr[:], in_=x_rows[:, :, 512 * c : 512 * (c + 1)])
             x_raw.append(xr)
 
@@ -86,11 +85,15 @@ def tile_attention_pa_kernel(tc, x, freqs_cis, wqkv_bytes, wqkv_scale, q_norm_w,
         warm = keep.tile([P, 1], F32, name="warm")
         nc.gpsimd.memset(warm[:], 1.0)
         warm2 = keep.tile([P, 1], F32, name="warm2")
-        nc.scalar.activation(out=warm2[:], in_=warm[:], func=ACT.Sqrt)
+        nc.scalar.activation(out=warm2[:], in_=warm[:], func=ACT.Abs_reciprocal_sqrt)
         ident_bf = keep.tile([P, P], BF16, name="ident_bf")
         make_identity(nc, ident_bf[:])
         ident = keep.tile([P, P], F32, name="ident")
         make_identity(nc, ident[:])
+
+        warm_ps = psum_t.tile([P, 512], F32, name="warm_ps", tag="tp")
+        for i in range(14):
+            nc.tensor.matmul(out=warm_ps[:, 0:P], lhsT=ident_bf[:], rhs=ident_bf[:], start=True, stop=True)
 
         gains_ps = psum_t.tile([P, 512], F32, name="gains_ps", tag="tp")
         gains = []
@@ -112,21 +115,23 @@ def tile_attention_pa_kernel(tc, x, freqs_cis, wqkv_bytes, wqkv_scale, q_norm_w,
                 in_=sp[:].rearrange("p (t n) -> p n t", t=4),
             )
 
-        tab_a = []
-        tab_b = []
+        tab = []
 
         def tables():
             g4 = []
             for qk in range(2):
                 g4.append(gains[qk][:].rearrange("p (j e) -> p j e", e=2).unsqueeze(1).to_broadcast([P, 2, 64, 2]))
             for qk in range(2):
-                ta = keep.tile([P, 2, 64, 2], F32, name="tab_a_%d" % qk)
-                nc.vector.tensor_tensor(out=ta[:], in0=g4[qk], in1=fc[:, :, :, 0:1].to_broadcast([P, 2, 64, 2]), op=ALU.mult)
-                tab_a.append(ta)
+                tab.append(keep.tile([P, 2, 2, 128], F32, name="tab_%d" % qk))
+                nc.vector.tensor_tensor(
+                    out=tab[qk][:, :, 0, :].rearrange("p t (j e) -> p t j e", e=2), in0=g4[qk],
+                    in1=fc[:, :, :, 0:1].to_broadcast([P, 2, 64, 2]), op=ALU.mult,
+                )
             for qk in range(2):
-                tb = keep.tile([P, 2, 64, 2], F32, name="tab_b_%d" % qk)
-                nc.vector.tensor_tensor(out=tb[:], in0=g4[qk], in1=fi_signed[:].rearrange("p e t j -> p t j e"), op=ALU.mult)
-                tab_b.append(tb)
+                nc.vector.tensor_tensor(
+                    out=tab[qk][:, :, 1, :].rearrange("p t (j e) -> p t j e", e=2), in0=g4[qk],
+                    in1=fi_signed[:].rearrange("p e t j -> p t j e"), op=ALU.mult,
+                )
 
         tables()
 
@@ -141,7 +146,6 @@ def tile_attention_pa_kernel(tc, x, freqs_cis, wqkv_bytes, wqkv_scale, q_norm_w,
         rope = {}
         sumsq = {}
         rstd = {}
-        roots = {}
         casts = {}
         sums = {}
 
@@ -263,45 +267,40 @@ def tile_attention_pa_kernel(tc, x, freqs_cis, wqkv_bytes, wqkv_scale, q_norm_w,
                 )
 
         def root(g):
-            rt = stat_pool.tile([P, 16], F32, name="root_%d" % g, tag="root")
-            nc.scalar.activation(out=rt[:], in_=sumsq[g][:], func=ACT.Sqrt, scale=1.0 / 128.0, bias=EPS)
-            roots[g] = rt
+            rstd[g] = stat_pool.tile([P, 16], F32, name="rstd_%d" % g, tag="rstd")
+            nc.scalar.activation(out=rstd[g][:], in_=sumsq[g][:], func=ACT.Abs_reciprocal_sqrt, scale=1.0 / 128.0, bias=EPS)
 
         def products(g, m):
             qk = 0 if g < 4 else 1
-            st = m % 2
-            a3 = acc[(g, m)][:].rearrange("p (h c) -> p h c", h=4)
-            t1 = sum_pool.tile([P, 512], F32, name="t1_%d_%d" % (g, m), tag="t1")
-            t2 = rope_pool.tile([P, 512], F32, name="t2_%d_%d" % (g, m), tag="t2")
-            ta = tab_a[qk][:, st, :, :].rearrange("p j e -> p (j e)").unsqueeze(1).to_broadcast([P, 4, 128])
-            tb = tab_b[qk][:, st, :, :].rearrange("p j e -> p (j e)").unsqueeze(1).to_broadcast([P, 4, 128])
-            nc.vector.tensor_tensor(out=t1[:].rearrange("p (h c) -> p h c", h=4), in0=a3, in1=ta, op=ALU.mult)
-            nc.vector.tensor_tensor(out=t2[:].rearrange("p (h c) -> p h c", h=4), in0=a3, in1=tb, op=ALU.mult)
-            rope[(g, m)] = (t1, t2)
+            t12 = sum_pool.tile([P, 2, 512], F32, name="t12_%d_%d" % (g, m), tag="t12")
+            nc.vector.tensor_tensor(
+                out=t12[:].rearrange("p z (h c) -> p z h c", h=4),
+                in0=acc[(g, m)][:].rearrange("p (h c) -> p h c", h=4).unsqueeze(1).to_broadcast([P, 2, 4, 128]),
+                in1=tab[qk][:, m % 2, :, :].unsqueeze(2).to_broadcast([P, 2, 4, 128]),
+                op=ALU.mult,
+            )
+            rope[(g, m)] = t12
 
         def combine(engine, g, m):
-            t1, t2 = rope[(g, m)]
+            t12 = rope[(g, m)]
             engine.tensor_tensor(
-                out=t1[:].rearrange("p (n e) -> p n e", e=2),
-                in0=t1[:].rearrange("p (n e) -> p n e", e=2),
-                in1=t2[:].rearrange("p (n e) -> p n e", e=2)[:, :, ::-1],
+                out=t12[:, 0, :].rearrange("p (n e) -> p n e", e=2),
+                in0=t12[:, 0, :].rearrange("p (n e) -> p n e", e=2),
+                in1=t12[:, 1, :].rearrange("p (n e) -> p n e", e=2)[:, :, ::-1],
                 op=ALU.add,
             )
 
         def add_on_tensor(g, m):
-            t1, t2 = rope[(g, m)]
+            t12 = rope[(g, m)]
             ps = psum_acc.tile([P, 512], F32, name="sum_%d_%d" % (g, m), tag="acc")
-            nc.tensor.matmul(out=ps[:], lhsT=ident[:], rhs=t1[:], start=True, stop=False)
+            nc.tensor.matmul(out=ps[:], lhsT=ident[:], rhs=t12[:, 0, :], start=True, stop=False)
             nc.tensor.matmul(
                 out=ps[:].rearrange("p (n e) -> p n e", e=2), lhsT=ident[:],
-                rhs=t2[:].rearrange("p (n e) -> p n e", e=2)[:, :, ::-1], start=False, stop=True,
+                rhs=t12[:, 1, :].rearrange("p (n e) -> p n e", e=2)[:, :, ::-1], start=False, stop=True,
             )
             sums[(g, m)] = ps
 
         def burst(g, follow):
-            if g == 4:
-                rstd[g] = stat_pool.tile([P, 16], F32, name="rstd_%d" % g, tag="rstd")
-                nc.vector.reciprocal(out=rstd[g][:], in_=roots[g][:])
             if g > 0:
                 if g < 3:
                     gate_col = 512 * V_PASSES[g + 2][1] - 1
@@ -313,9 +312,6 @@ def tile_attention_pa_kernel(tc, x, freqs_cis, wqkv_bytes, wqkv_scale, q_norm_w,
                 products(g, m)
                 if m < 2:
                     combine(nc.gpsimd, g, m)
-                if m == 2 and g < 4:
-                    rstd[g] = stat_pool.tile([P, 16], F32, name="rstd_%d" % g, tag="rstd")
-                    nc.vector.reciprocal(out=rstd[g][:], in_=roots[g][:])
                 if follow is not None:
                     follow(m)
             if g >= 3:
@@ -325,7 +321,7 @@ def tile_attention_pa_kernel(tc, x, freqs_cis, wqkv_bytes, wqkv_scale, q_norm_w,
             o = out_pool.tile([P, 512], F32, name="o_%d_%d" % (g, m), tag="o")
             for h in range(4):
                 nc.scalar.activation(
-                    out=o[:, P * h : P * (h + 1)], in_=sums.get((g, m), rope[(g, m)][0])[:, P * h : P * (h + 1)], func=ACT.Copy,
+                    out=o[:, P * h : P * (h + 1)], in_=sums[(g, m)][:, P * h : P * (h + 1)] if (g, m) in sums else rope[(g, m)][:, 0, P * h : P * (h + 1)], func=ACT.Copy,
                     scale=rstd[g][:, 4 * m + h : 4 * m + h + 1],
                 )
             store(g, m, o[:])
@@ -334,7 +330,7 @@ def tile_attention_pa_kernel(tc, x, freqs_cis, wqkv_bytes, wqkv_scale, q_norm_w,
             o = out_pool.tile([P, 512], F32, name="o_%d_%d" % (g, m), tag="o")
             nc.vector.tensor_tensor(
                 out=o[:].rearrange("p (h c) -> p h c", h=4),
-                in0=rope[(g, m)][0][:].rearrange("p (h c) -> p h c", h=4),
+                in0=rope[(g, m)][:, 0, :].rearrange("p (h c) -> p h c", h=4),
                 in1=rstd[g][:, 4 * m : 4 * (m + 1)].unsqueeze(2).to_broadcast([P, 4, 128]),
                 op=ALU.mult,
             )

@@ -292,7 +292,10 @@ def tile_attention_pa_kernel(tc, x, freqs_cis, wqkv_bytes, wqkv_scale, q_norm_w,
 
         def add_on_tensor(g, m):
             t12 = rope[(g, m)]
-            ps = psum_acc.tile([P, 512], F32, name="sum_%d_%d" % (g, m), tag="acc")
+            if g < 3:
+                ps = psum_acc.tile([P, 512], F32, name="sum_%d_%d" % (g, m), tag="acc")
+            else:
+                ps = psum_t.tile([P, 512], F32, name="sum_%d_%d" % (g, m), tag="tp")
             nc.tensor.matmul(out=ps[:], lhsT=ident[:], rhs=t12[:, 0, :], start=True, stop=False)
             nc.tensor.matmul(
                 out=ps[:].rearrange("p (n e) -> p n e", e=2), lhsT=ident[:],
@@ -314,7 +317,7 @@ def tile_attention_pa_kernel(tc, x, freqs_cis, wqkv_bytes, wqkv_scale, q_norm_w,
                     combine(nc.gpsimd, g, m)
                 if follow is not None:
                     follow(m)
-            if g >= 3:
+            if g == 4:
                 combine(nc.vector, g, 2)
 
         def finish(g, m):
@@ -359,6 +362,8 @@ def tile_attention_pa_kernel(tc, x, freqs_cis, wqkv_bytes, wqkv_scale, q_norm_w,
             return 4 * g + 11 if g < 4 else 25
 
         def finish_tick(g, m):
+            if (g == 2 and m < 2) or (g == 1 and m == 3):
+                return 22
             return burst_tick(g) + 1 if m < 3 else burst_tick(g + 1) + 1
 
         def multiply_tick(g, m):
@@ -378,7 +383,7 @@ def tile_attention_pa_kernel(tc, x, freqs_cis, wqkv_bytes, wqkv_scale, q_norm_w,
             for k in range(UNITS):
                 if turn_tick(k) == tick:
                     turn(k)
-            for g in range(3):
+            for g in range(4):
                 if burst_tick(g) + 1 == tick:
                     add_on_tensor(g, 2)
             for g in range(GROUPS):

@@ -273,12 +273,15 @@ def tile_attention_pa_kernel(tc, x, freqs_cis, wqkv_bytes, wqkv_scale, q_norm_w,
         def products(g, m):
             qk = 0 if g < 4 else 1
             t12 = sum_pool.tile([P, 2, 512], F32, name="t12_%d_%d" % (g, m), tag="t12")
-            nc.vector.tensor_tensor(
-                out=t12[:].rearrange("p z (h c) -> p z h c", h=4),
-                in0=acc[(g, m)][:].rearrange("p (h c) -> p h c", h=4).unsqueeze(1).to_broadcast([P, 2, 4, 128]),
-                in1=tab[qk][:, m % 2, :, :].unsqueeze(2).to_broadcast([P, 2, 4, 128]),
-                op=ALU.mult,
-            )
+            for h in range(4):
+                head = slice(P * h, P * (h + 1))
+                nc.vector.scalar_tensor_tensor(
+                    out=t12[:, :, head],
+                    in0=acc[(g, m)][:, head].unsqueeze(1).to_broadcast([P, 2, 128]),
+                    scalar=rstd[g][:, 4 * m + h : 4 * m + h + 1],
+                    in1=tab[qk][:, m % 2, :, :],
+                    op0=ALU.mult, op1=ALU.mult,
+                )
             rope[(g, m)] = t12
 
         def combine(engine, g, m):
@@ -289,6 +292,7 @@ def tile_attention_pa_kernel(tc, x, freqs_cis, wqkv_bytes, wqkv_scale, q_norm_w,
                 in1=t12[:, 1, :].rearrange("p (n e) -> p n e", e=2)[:, :, ::-1],
                 op=ALU.add,
             )
+            store(g, m, t12[:, 0, :])
 
         def add_on_tensor(g, m):
             t12 = rope[(g, m)]
@@ -322,21 +326,7 @@ def tile_attention_pa_kernel(tc, x, freqs_cis, wqkv_bytes, wqkv_scale, q_norm_w,
 
         def finish(g, m):
             o = out_pool.tile([P, 512], F32, name="o_%d_%d" % (g, m), tag="o")
-            for h in range(4):
-                nc.scalar.activation(
-                    out=o[:, P * h : P * (h + 1)], in_=sums[(g, m)][:, P * h : P * (h + 1)] if (g, m) in sums else rope[(g, m)][:, 0, P * h : P * (h + 1)], func=ACT.Copy,
-                    scale=rstd[g][:, 4 * m + h : 4 * m + h + 1],
-                )
-            store(g, m, o[:])
-
-        def finish_on_vector(g, m):
-            o = out_pool.tile([P, 512], F32, name="o_%d_%d" % (g, m), tag="o")
-            nc.vector.tensor_tensor(
-                out=o[:].rearrange("p (h c) -> p h c", h=4),
-                in0=rope[(g, m)][:, 0, :].rearrange("p (h c) -> p h c", h=4),
-                in1=rstd[g][:, 4 * m : 4 * (m + 1)].unsqueeze(2).to_broadcast([P, 4, 128]),
-                op=ALU.mult,
-            )
+            nc.scalar.copy(out=o[:], in_=sums[(g, m)][:])
             store(g, m, o[:])
 
         def plain_out(g, m):
@@ -360,11 +350,6 @@ def tile_attention_pa_kernel(tc, x, freqs_cis, wqkv_bytes, wqkv_scale, q_norm_w,
 
         def burst_tick(g):
             return 4 * g + 11 if g < 4 else 25
-
-        def finish_tick(g, m):
-            if (g == 2 and m < 2) or (g == 1 and m == 3):
-                return 22
-            return burst_tick(g) + 1 if m < 3 else burst_tick(g + 1) + 1
 
         def multiply_tick(g, m):
             return 4 * g + 8 + m // 2
@@ -390,9 +375,8 @@ def tile_attention_pa_kernel(tc, x, freqs_cis, wqkv_bytes, wqkv_scale, q_norm_w,
                 if max(4 * g - 1, 2) == tick and V_PASSES[g][1] - V_PASSES[g][0] < PASSES:
                     cast(g)
             for g in range(4):
-                for m in range(TOK_TILES):
-                    if finish_tick(g, m) == tick:
-                        finish(g, m)
+                if burst_tick(g) + 1 == tick:
+                    finish(g, 2)
             for k in range(UNITS):
                 if quantize_tick(k) == tick:
                     quantize(k)
@@ -410,13 +394,6 @@ def tile_attention_pa_kernel(tc, x, freqs_cis, wqkv_bytes, wqkv_scale, q_norm_w,
                 if burst_tick(g) == tick:
                     burst(g, next_group if g == 3 else None)
             if tick == 25:
-                finish(3, 3)
-                plain_out(5, 0)
-                finish(4, 0)
-                plain_out(5, 1)
-                finish(4, 1)
-                plain_out(5, 2)
-                plain_out(5, 3)
+                for m in range(TOK_TILES):
+                    plain_out(5, m)
                 combine(nc.vector, 4, 3)
-                finish_on_vector(4, 2)
-                finish_on_vector(4, 3)

@@ -23,8 +23,12 @@ GROUPS = 6
 ROPE_GROUPS = 5
 UNITS = 4 + 4 * GROUPS
 EPS = 1e-6
-MANUAL = True
-V_PASSES = ((2, 4), (2, 3), (2, 3), (2, 3), (2, 4), (0, 4))
+S_PASS = 3
+S_GROUPS = (1, 2, 3, 4, 5)
+V_CASTS = (5,)
+S_CAST = (0, 1, 3, 11, 15, 19)
+S_TURN = (0, 2, 9, 13, 17, 21)
+S_QUANT = (0, 5, 11, 15, 19, 99)
 
 
 def tile_attention_pa_kernel(tc, x, freqs_cis, wqkv_bytes, wqkv_scale, q_norm_w, k_norm_w, out_0, out_1, out_2):
@@ -41,15 +45,15 @@ def tile_attention_pa_kernel(tc, x, freqs_cis, wqkv_bytes, wqkv_scale, q_norm_w,
         bytes_pool = ctx.enter_context(tc.tile_pool(name="bytes_pool", bufs=ROW_TILES))
         wide_pool = ctx.enter_context(tc.tile_pool(name="wide_pool", bufs=8))
         cast_pool = ctx.enter_context(tc.tile_pool(name="cast_pool", bufs=2))
+        plane_pool = ctx.enter_context(tc.tile_pool(name="plane_pool", bufs=4))
         grouped_pool = ctx.enter_context(tc.tile_pool(name="grouped_pool", bufs=7))
         codes_pool = ctx.enter_context(tc.tile_pool(name="codes_pool", bufs=3))
         sum_pool = ctx.enter_context(tc.tile_pool(name="sum_pool", bufs=8))
-        out_pool = ctx.enter_context(tc.tile_pool(name="out_pool", bufs=10))
+        out_pool = ctx.enter_context(tc.tile_pool(name="out_pool", bufs=4))
         stat_pool = ctx.enter_context(tc.tile_pool(name="stat_pool", bufs=3))
         psum_t = ctx.enter_context(tc.psum_pool(name="psum_t", bufs=4))
         psum_acc = ctx.enter_context(tc.psum_pool(name="psum_acc", bufs=4))
-        if MANUAL:
-            ctx.enter_context(tc.manual_schedule())
+        ctx.enter_context(tc.manual_schedule())
 
         scale_col = keep.tile([P, 16], F32, name="scale_col")
         nc.sync.dma_start(out=scale_col[:].rearrange("p (g t) -> p g t", t=4), in_=wqkv_scale.rearrange("o (g p t) -> p (o g) t", p=P, t=4))
@@ -61,25 +65,30 @@ def tile_attention_pa_kernel(tc, x, freqs_cis, wqkv_bytes, wqkv_scale, q_norm_w,
             nc.scalar.dma_start(out=g_c[:], in_=vec.rearrange("(p o) -> p o", o=1))
             gain_col.append(g_c)
 
-        w_bytes = []
-        x_raw = []
+        w_bytes = {}
+        x_raw = {}
 
         def load_w(t):
             wb = bytes_pool.tile([P, D], U8, name="w_bytes_%d" % t, tag="w_bytes")
             nc.sync.dma_start(out=wb[:], in_=wqkv_bytes[P * t : P * (t + 1), :])
-            w_bytes.append(wb)
+            w_bytes[t] = wb
 
         def load_x(c):
             xr = wide_pool.tile([P, TOK_TILES, 512], BF16, name="x_raw_%d" % c, tag="wide")
             nc.sync.dma_start(out=xr[:], in_=x_rows[:, :, 512 * c : 512 * (c + 1)])
-            x_raw.append(xr)
+            x_raw[c] = xr
 
         load_w(0)
+        load_x(0)
         load_w(1)
-        for c in range(PASSES):
-            load_x(c)
-            load_w(2 + c)
-        for t in range(6, ROW_TILES):
+        load_x(1)
+        for t in range(4, 8):
+            load_w(t)
+        load_w(2)
+        load_x(2)
+        load_w(3)
+        load_x(3)
+        for t in range(8, ROW_TILES):
             load_w(t)
 
         warm = keep.tile([P, 1], F32, name="warm")
@@ -147,16 +156,19 @@ def tile_attention_pa_kernel(tc, x, freqs_cis, wqkv_bytes, wqkv_scale, q_norm_w,
         sumsq = {}
         rstd = {}
         casts = {}
+        dead = []
+        planes = {}
+        s_banks = {}
         sums = {}
 
         def widen(t):
             wd = wide_pool.tile([P, D], BF16, name="wide_%d" % t, tag="wide")
-            pieces = 4 if t == 0 else 1
-            first, last = (512 * V_PASSES[t // 4][0], 512 * V_PASSES[t // 4][1]) if t % 4 == 3 else (0, D)
-            width = (last - first) // pieces
-            for c in range(pieces if last > first else 0):
-                cols = slice(first + width * c, first + width * (c + 1))
+            last = 512 * S_PASS if t // 4 in S_GROUPS else D
+            width = 512 if t == 0 else last
+            for first in range(0, last, width):
+                cols = slice(first, first + width)
                 nc.vector.tensor_tensor(out=wd[:, cols], in0=w_bytes[t][:, cols].bitcast(FP8), in1=scale_b[:, cols], op=ALU.mult)
+                dead.append(w_bytes[t][:, first + width - 1 : first + width])
             wide[t] = wd
 
         def widen_last(c):
@@ -165,71 +177,86 @@ def tile_attention_pa_kernel(tc, x, freqs_cis, wqkv_bytes, wqkv_scale, q_norm_w,
                 if c == 0:
                     wide[t] = wide_pool.tile([P, D], BF16, name="wide_%d" % t, tag="wide")
                 nc.vector.tensor_tensor(out=wide[t][:, cols], in0=w_bytes[t][:, cols].bitcast(FP8), in1=scale_b[:, cols], op=ALU.mult)
+                dead.append(w_bytes[t][:, 512 * c + 511 : 512 * (c + 1)])
 
-        def cast(g):
-            cs = cast_pool.tile([P, D], BF16, name="cast_%d" % g, tag="cast")
-            for a, b in ((0, 512 * V_PASSES[g][0]), (512 * V_PASSES[g][1], D)):
-                if b > a:
-                    nc.scalar.copy(out=cs[:, a:b], in_=w_bytes[4 * g + 3][:, a:b].bitcast(FP8))
-            casts[g] = cs
+        def cast(g, j):
+            if j == 0:
+                casts[g] = cast_pool.tile([P, 4, 512], BF16, name="cast_%d" % g, tag="cast")
+            if g in V_CASTS:
+                nc.vector.tensor_copy(out=casts[g][:, j, :], in_=w_bytes[4 * g + j][:, 512 * S_PASS : 512 * (S_PASS + 1)].bitcast(FP8))
+                dead.append(w_bytes[4 * g + j][:, D - 1 : D])
+            else:
+                nc.scalar.copy(out=casts[g][:, j, :], in_=w_bytes[4 * g + j][:, 512 * S_PASS : 512 * (S_PASS + 1)].bitcast(FP8))
 
         def unit_words(k, j):
             if k < PASSES:
                 return x_raw[k][:, j, :].bitcast(F32)
             g, p = divmod(k - PASSES, PASSES)
+            if g in S_GROUPS and p == S_PASS:
+                return casts[g][:, j, :].bitcast(F32)
             return wide[4 * g + j][:].bitcast(F32)[:, 256 * p : 256 * (p + 1)]
 
-        def turn(k):
-            gr = grouped_pool.tile([P, D], BF16, name="grouped_%d" % k, tag="grouped", align_bytes=64)
-            grouped[k] = gr
-            g, p = divmod(k - PASSES, PASSES)
-            by_scalar = k >= PASSES and not V_PASSES[g][0] <= p < V_PASSES[g][1]
+        def transposes(k):
             banks = []
             for pair in range(2):
                 tp = psum_t.tile([P, 512], F32, name="tp_%d_%d" % (k, pair), tag="tp")
                 banks.append(tp)
-                if pair == 1 and by_scalar:
-                    words = unit_words(k, 2)
+                for jj in range(2):
+                    words = unit_words(k, 2 * pair + jj)
                     for u in range(2):
-                        nc.tensor.transpose(tp[:, P * u : P * (u + 1)], words[:, u : 256 : 2], ident[:])
-                    planes = tp[:, 256:512].bitcast(BF16)
-                    for t in range(4):
-                        nc.tensor.transpose(planes[:, P * t : P * (t + 1)], casts[g][:, 512 * p + t : 512 * (p + 1) : 4], ident_bf[:])
-                else:
-                    for jj in range(2):
-                        words = unit_words(k, 2 * pair + jj)
-                        for u in range(2):
-                            nc.tensor.transpose(tp[:, 256 * u + P * jj : 256 * u + P * (jj + 1)], words[:, u : 256 : 2], ident[:])
+                        nc.tensor.transpose(tp[:, 256 * u + P * jj : 256 * u + P * (jj + 1)], words[:, u : 256 : 2], ident[:])
+            return banks
+
+        def turn(k):
+            gr = grouped_pool.tile([P, D], BF16, name="grouped_%d" % k, tag="grouped", align_bytes=64)
+            grouped[k] = gr
+            banks = transposes(k)
             for pair in range(2):
-                if pair == 1 and by_scalar:
-                    nc.scalar.copy(
-                        out=gr[:, 1024:1536].bitcast(F32).rearrange("p (n u) -> p n u", u=2),
-                        in_=banks[1][:, 0:256].rearrange("p (u n) -> p n u", u=2),
+                nc.scalar.copy(
+                    out=gr[:, 1024 * pair : 1024 * (pair + 1)].bitcast(F32).rearrange("p (n u) -> p n u", u=2),
+                    in_=banks[pair][:].rearrange("p (u n) -> p n u", u=2),
+                )
+
+        def turn_s(g):
+            k = PASSES + PASSES * g + S_PASS
+            banks = transposes(k)
+            s_banks[g] = banks
+            for pair in range(2):
+                pl = plane_pool.tile([P, 4, 256], BF16, name="planes_%d_%d" % (g, pair), tag="planes")
+                planes[(g, pair)] = pl
+                view = banks[pair][:].bitcast(BF16).rearrange("p (u n e) -> p u n e", u=2, e=2)
+                for t in range(4):
+                    nc.scalar.activation(
+                        out=pl[:, t, :], in_=view[:, t // 2, :, t % 2], func=ACT.Copy,
+                        scale=scale_col[:, 4 * S_PASS + t : 4 * S_PASS + t + 1],
                     )
-                    planes = banks[1][:, 256:512].bitcast(BF16)
-                    for t in range(4):
-                        nc.scalar.activation(
-                            out=gr[:, 1536:2048].rearrange("p (n t) -> p n t", t=4)[:, :, t : t + 1],
-                            in_=planes[:, P * t : P * (t + 1)].unsqueeze(2),
-                            func=ACT.Copy,
-                            scale=scale_col[:, 4 * p + t : 4 * p + t + 1],
-                        )
-                else:
-                    nc.scalar.copy(
-                        out=gr[:, 1024 * pair : 1024 * (pair + 1)].bitcast(F32).rearrange("p (n u) -> p n u", u=2),
-                        in_=banks[pair][:].rearrange("p (u n) -> p n u", u=2),
+
+        def stage_b(g):
+            k = PASSES + PASSES * g + S_PASS
+            gr = grouped_pool.tile([P, D], BF16, name="grouped_%d" % k, tag="grouped", align_bytes=64)
+            grouped[k] = gr
+            for pair in range(2):
+                for h in range(2):
+                    nc.tensor.matmul(
+                        out=s_banks[g][pair][:].bitcast(BF16)[:, 512 * h : 512 * (h + 1)].rearrange("p (n t) -> p n t", t=4),
+                        lhsT=ident_bf[:],
+                        rhs=planes[(g, pair)][:, :, P * h : P * (h + 1)].rearrange("p t n -> p n t"),
+                        start=True, stop=True,
                     )
+            for pair in range(2):
+                nc.scalar.copy(out=gr[:, 1024 * pair : 1024 * (pair + 1)].bitcast(F32), in_=s_banks[g][pair][:])
 
         def quantize(k):
             if k < PASSES:
                 codes, scales = x_codes[:, k, :], x_scales[:, k, :]
             else:
                 g, p = divmod(k - PASSES, PASSES)
-                if p == 0:
-                    w_codes[g] = codes_pool.tile([P, PASSES, 512], U32, name="w_codes_%d" % g, tag="w_codes", align_bytes=64)
-                    w_scales[g] = codes_pool.tile([P, PASSES, 512], U8, name="w_scales_%d" % g, tag="w_scales", align_bytes=64)
+                for n in range(len(w_codes), g + 1):
+                    w_codes[n] = codes_pool.tile([P, PASSES, 512], U32, name="w_codes_%d" % n, tag="w_codes", align_bytes=64)
+                    w_scales[n] = codes_pool.tile([P, PASSES, 512], U8, name="w_scales_%d" % n, tag="w_scales", align_bytes=64)
                 codes, scales = w_codes[g][:, p, :], w_scales[g][:, p, :]
             nc.vector.quantize_mx(out=codes.bitcast(FP8X4), scales=scales, in_=grouped[k][:])
+            dead.append(grouped[k][:, 0:1])
 
         def multiply(g, m):
             if g < ROPE_GROUPS:
@@ -254,7 +281,7 @@ def tile_attention_pa_kernel(tc, x, freqs_cis, wqkv_bytes, wqkv_scale, q_norm_w,
                 dst = outs[0][rows, 512 * g : 512 * (g + 1)]
             else:
                 dst = outs[g - 3][rows, :]
-            nc.sync.dma_start(out=dst, in_=tile_ap)
+            (nc.scalar if g == 5 else nc.sync).dma_start(out=dst, in_=tile_ap)
 
         def squares(g, m):
             if m == 0:
@@ -266,9 +293,11 @@ def tile_attention_pa_kernel(tc, x, freqs_cis, wqkv_bytes, wqkv_scale, q_norm_w,
                     accum_out=sumsq[g][:, 4 * m + h : 4 * m + h + 1],
                 )
 
-        def root(g):
-            rstd[g] = stat_pool.tile([P, 16], F32, name="rstd_%d" % g, tag="rstd")
-            nc.scalar.activation(out=rstd[g][:], in_=sumsq[g][:], func=ACT.Abs_reciprocal_sqrt, scale=1.0 / 128.0, bias=EPS)
+        def root(g, first, last):
+            if first == 0:
+                rstd[g] = stat_pool.tile([P, 16], F32, name="rstd_%d" % g, tag="rstd")
+            cols = slice(4 * first, 4 * last)
+            nc.scalar.activation(out=rstd[g][:, cols], in_=sumsq[g][:, cols], func=ACT.Abs_reciprocal_sqrt, scale=1.0 / 128.0, bias=EPS)
 
         def products(g, m):
             qk = 0 if g < 4 else 1
@@ -296,10 +325,7 @@ def tile_attention_pa_kernel(tc, x, freqs_cis, wqkv_bytes, wqkv_scale, q_norm_w,
 
         def add_on_tensor(g, m):
             t12 = rope[(g, m)]
-            if g < 3:
-                ps = psum_acc.tile([P, 512], F32, name="sum_%d_%d" % (g, m), tag="acc")
-            else:
-                ps = psum_t.tile([P, 512], F32, name="sum_%d_%d" % (g, m), tag="tp")
+            ps = psum_t.tile([P, 512], F32, name="sum_%d_%d" % (g, m), tag="tp")
             nc.tensor.matmul(out=ps[:], lhsT=ident[:], rhs=t12[:, 0, :], start=True, stop=False)
             nc.tensor.matmul(
                 out=ps[:].rearrange("p (n e) -> p n e", e=2), lhsT=ident[:],
@@ -308,21 +334,17 @@ def tile_attention_pa_kernel(tc, x, freqs_cis, wqkv_bytes, wqkv_scale, q_norm_w,
             sums[(g, m)] = ps
 
         def burst(g, follow):
-            if g > 0:
-                if g < 3:
-                    gate_col = 512 * V_PASSES[g + 2][1] - 1
-                    nc.gpsimd.memset(w_bytes[4 * g + 11][:, gate_col : gate_col + 1], 0)
-                else:
-                    nc.gpsimd.memset(grouped[22 if g == 3 else 26][:, 0:1], 0.0)
-                combine(nc.gpsimd, g - 1, 3)
+            late = {0: (), 4: ((3, 2), (3, 3))}.get(g, ((g - 1, 3),))
+            if late:
+                nc.gpsimd.memset(dead[-2], 0.0 if dead[-2].dtype == BF16 else 0)
+            for bank in late:
+                combine(nc.gpsimd, bank[0], bank[1])
             for m in range(TOK_TILES):
                 products(g, m)
-                if m < 2:
+                if m < (1 if g == 4 else 2):
                     combine(nc.gpsimd, g, m)
                 if follow is not None:
                     follow(m)
-            if g == 4:
-                combine(nc.vector, g, 2)
 
         def finish(g, m):
             o = out_pool.tile([P, 512], F32, name="o_%d_%d" % (g, m), tag="o")
@@ -334,66 +356,79 @@ def tile_attention_pa_kernel(tc, x, freqs_cis, wqkv_bytes, wqkv_scale, q_norm_w,
             nc.scalar.copy(out=o[:], in_=acc[(g, m)][:])
             store(g, m, o[:])
 
-        def turn_tick(k):
-            if k < PASSES:
-                return k + 1
-            if k <= 23:
-                return k - 1
-            return (21, 22, 23, 23)[k - 24]
+        def unit(g, p):
+            return PASSES + PASSES * g + p
 
-        def quantize_tick(k):
-            if k < PASSES:
-                return k + 3
-            if k <= 22:
-                return k + 1
-            return 23 if k == 23 else 24
+        def follow(g):
+            def f(m):
+                if 0 <= g + 1 < ROPE_GROUPS:
+                    multiply(g + 1, m)
+                    squares(g + 1, m)
+                    if g + 1 == 4:
+                        root(4, m, m + 1)
+                    elif m == 3:
+                        root(g + 1, 0, 4)
+            return f
 
-        def burst_tick(g):
-            return 4 * g + 11 if g < 4 else 25
 
-        def multiply_tick(g, m):
-            return 4 * g + 8 + m // 2
-
-        def next_group(m):
-            multiply(4, m)
-            squares(4, m)
-            if m == 3:
-                root(4)
-
-        for tick in range(26):
+        for tick in range(24):
+            a, phase = divmod(tick - 3, 4)
             if tick < 20:
                 widen(tick)
-            elif tick < ROW_TILES:
+            elif tick - 20 != S_PASS:
                 widen_last(tick - 20)
-            for k in range(UNITS):
-                if turn_tick(k) == tick:
-                    turn(k)
-            for g in range(4):
-                if burst_tick(g) + 1 == tick:
-                    add_on_tensor(g, 2)
-            for g in range(GROUPS):
-                if max(4 * g - 1, 2) == tick and V_PASSES[g][1] - V_PASSES[g][0] < PASSES:
-                    cast(g)
-            for g in range(4):
-                if burst_tick(g) + 1 == tick:
-                    finish(g, 2)
-            for k in range(UNITS):
-                if quantize_tick(k) == tick:
-                    quantize(k)
-            for g in range(4):
-                for m in range(TOK_TILES):
-                    if multiply_tick(g, m) == tick:
-                        multiply(g, m)
-                        squares(g, m)
-                        if m == 3:
-                            root(g)
-            if tick == 24:
+            if tick in (1, 2):
+                turn(2 * tick - 2)
+                turn(2 * tick - 1)
+            if tick in (3, 4):
+                quantize(2 * tick - 6)
+                quantize(2 * tick - 5)
+            if tick == 7:
+                quantize(unit(0, 3))
+            for g in S_GROUPS:
+                if S_TURN[g] + 1 == tick:
+                    stage_b(g)
+            if phase == 0 and 0 <= a <= 4:
+                for p in range(PASSES):
+                    if not (a in S_GROUPS and p == S_PASS):
+                        turn(unit(a, p))
+                if a >= 2:
+                    burst(a - 2, follow(a - 2))
+                else:
+                    for m in range(TOK_TILES):
+                        follow(a - 2)(m)
+            if phase == 1:
+                if a >= 2:
+                    add_on_tensor(a - 2, 2)
+                    finish(a - 2, 2)
+            for g in S_GROUPS:
+                if S_TURN[g] == tick:
+                    turn_s(g)
+            for g in S_GROUPS:
+                if S_CAST[g] == tick:
+                    for j in range(4):
+                        cast(g, j)
+            if 20 <= tick <= 22:
+                turn(unit(5, tick - 20))
+            if a == 0:
+                if phase == 2:
+                    quantize(unit(1, S_PASS))
+                    quantize(unit(0, 0))
+                if phase == 3:
+                    quantize(unit(0, 1))
+                    quantize(unit(0, 2))
+            elif phase > 0 and a > 0:
+                quantize(unit(a, phase - 1))
+            for g in S_GROUPS:
+                if S_QUANT[g] == tick and g > 1:
+                    quantize(unit(g, S_PASS))
+            if tick == 23:
+                burst(3, follow(3))
+                for p in (0, S_PASS, 1, 2):
+                    quantize(unit(5, p))
                 for m in range(TOK_TILES):
                     multiply(5, m)
-            for g in range(ROPE_GROUPS):
-                if burst_tick(g) == tick:
-                    burst(g, next_group if g == 3 else None)
-            if tick == 25:
-                for m in range(TOK_TILES):
                     plain_out(5, m)
-                combine(nc.vector, 4, 3)
+                burst(4, None)
+                for m in range(1, TOK_TILES):
+                    combine(nc.vector, 4, m)

@@ -25,7 +25,7 @@ UNITS = 4 + 4 * GROUPS
 EPS = 1e-6
 S_PASS = 3
 S_GROUPS = (1, 2, 3, 4, 5)
-V_CASTS = (5,)
+V_CASTS = ()
 S_CAST = (0, 1, 3, 11, 15, 19)
 S_TURN = (0, 2, 9, 13, 17, 21)
 S_QUANT = (0, 5, 11, 15, 19, 99)
@@ -222,12 +222,12 @@ def tile_attention_pa_kernel(tc, x, freqs_cis, wqkv_bytes, wqkv_scale, q_norm_w,
             banks = transposes(k)
             s_banks[g] = banks
             for pair in range(2):
-                pl = plane_pool.tile([P, 4, 256], BF16, name="planes_%d_%d" % (g, pair), tag="planes")
+                pl = plane_pool.tile([P, 32, 4, 8], BF16, name="planes_%d_%d" % (g, pair), tag="planes")
                 planes[(g, pair)] = pl
-                view = banks[pair][:].bitcast(BF16).rearrange("p (u n e) -> p u n e", u=2, e=2)
+                view = banks[pair][:].bitcast(BF16).rearrange("p (u a b e) -> p u a b e", u=2, b=8, e=2)
                 for t in range(4):
                     nc.scalar.activation(
-                        out=pl[:, t, :], in_=view[:, t // 2, :, t % 2], func=ACT.Copy,
+                        out=pl[:, :, t, :], in_=view[:, t // 2, :, :, t % 2], func=ACT.Copy,
                         scale=scale_col[:, 4 * S_PASS + t : 4 * S_PASS + t + 1],
                     )
 
@@ -238,9 +238,9 @@ def tile_attention_pa_kernel(tc, x, freqs_cis, wqkv_bytes, wqkv_scale, q_norm_w,
             for pair in range(2):
                 for h in range(2):
                     nc.tensor.matmul(
-                        out=s_banks[g][pair][:].bitcast(BF16)[:, 512 * h : 512 * (h + 1)].rearrange("p (n t) -> p n t", t=4),
+                        out=s_banks[g][pair][:].bitcast(BF16)[:, 512 * h : 512 * (h + 1)].rearrange("p (a b t) -> p a b t", b=8, t=4),
                         lhsT=ident_bf[:],
-                        rhs=planes[(g, pair)][:, :, P * h : P * (h + 1)].rearrange("p t n -> p n t"),
+                        rhs=planes[(g, pair)][:, 16 * h : 16 * (h + 1), :, :].rearrange("p a t b -> p a b t"),
                         start=True, stop=True,
                     )
             for pair in range(2):
@@ -361,6 +361,10 @@ def tile_attention_pa_kernel(tc, x, freqs_cis, wqkv_bytes, wqkv_scale, q_norm_w,
 
         def follow(g):
             def f(m):
+                if m == 1 and g + 2 <= 5:
+                    for p in range(2, PASSES):
+                        if not (g + 2 in S_GROUPS and p == S_PASS):
+                            turn(unit(g + 2, p))
                 if 0 <= g + 1 < ROPE_GROUPS:
                     multiply(g + 1, m)
                     squares(g + 1, m)
@@ -368,15 +372,14 @@ def tile_attention_pa_kernel(tc, x, freqs_cis, wqkv_bytes, wqkv_scale, q_norm_w,
                         root(4, m, m + 1)
                     elif m == 3:
                         root(g + 1, 0, 4)
+                if g + 3 >= 3 and g + 3 in S_GROUPS and g + 3 not in V_CASTS:
+                    cast(g + 3, m)
             return f
 
 
         for tick in range(24):
             a, phase = divmod(tick - 3, 4)
-            if tick < 20:
-                widen(tick)
-            elif tick - 20 != S_PASS:
-                widen_last(tick - 20)
+            widen(tick)
             if tick in (1, 2):
                 turn(2 * tick - 2)
                 turn(2 * tick - 1)
@@ -389,9 +392,8 @@ def tile_attention_pa_kernel(tc, x, freqs_cis, wqkv_bytes, wqkv_scale, q_norm_w,
                 if S_TURN[g] + 1 == tick:
                     stage_b(g)
             if phase == 0 and 0 <= a <= 4:
-                for p in range(PASSES):
-                    if not (a in S_GROUPS and p == S_PASS):
-                        turn(unit(a, p))
+                turn(unit(a, 0))
+                turn(unit(a, 1))
                 if a >= 2:
                     burst(a - 2, follow(a - 2))
                 else:
@@ -405,11 +407,9 @@ def tile_attention_pa_kernel(tc, x, freqs_cis, wqkv_bytes, wqkv_scale, q_norm_w,
                 if S_TURN[g] == tick:
                     turn_s(g)
             for g in S_GROUPS:
-                if S_CAST[g] == tick:
+                if S_CAST[g] == tick and (g < 3 or g in V_CASTS):
                     for j in range(4):
                         cast(g, j)
-            if 20 <= tick <= 22:
-                turn(unit(5, tick - 20))
             if a == 0:
                 if phase == 2:
                     quantize(unit(1, S_PASS))
@@ -423,6 +423,8 @@ def tile_attention_pa_kernel(tc, x, freqs_cis, wqkv_bytes, wqkv_scale, q_norm_w,
                 if S_QUANT[g] == tick and g > 1:
                     quantize(unit(g, S_PASS))
             if tick == 23:
+                turn(unit(5, 0))
+                turn(unit(5, 1))
                 burst(3, follow(3))
                 for p in (0, S_PASS, 1, 2):
                     quantize(unit(5, p))

@@ -345,6 +345,8 @@ def tile_attention_pa_kernel(tc, x, freqs_cis, wqkv_bytes, wqkv_scale, q_norm_w,
                     combine(nc.gpsimd, g, m)
                 if follow is not None:
                     follow(m)
+            if g < 3:
+                combine(nc.vector, g, 2)
 
         def finish(g, m):
             o = out_pool.tile([P, 512], F32, name="o_%d_%d" % (g, m), tag="o")
@@ -399,10 +401,6 @@ def tile_attention_pa_kernel(tc, x, freqs_cis, wqkv_bytes, wqkv_scale, q_norm_w,
                 else:
                     for m in range(TOK_TILES):
                         follow(a - 2)(m)
-            if phase == 1:
-                if a >= 2:
-                    add_on_tensor(a - 2, 2)
-                    finish(a - 2, 2)
             for g in S_GROUPS:
                 if S_TURN[g] == tick:
                     turn_s(g)

@@ -222,12 +222,12 @@ def tile_attention_pa_kernel(tc, x, freqs_cis, wqkv_bytes, wqkv_scale, q_norm_w,
             banks = transposes(k)
             s_banks[g] = banks
             for pair in range(2):
-                pl = plane_pool.tile([P, 32, 4, 8], BF16, name="planes_%d_%d" % (g, pair), tag="planes")
+                pl = plane_pool.tile([P, 2, 256, 2], BF16, name="planes_%d_%d" % (g, pair), tag="planes")
                 planes[(g, pair)] = pl
-                view = banks[pair][:].bitcast(BF16).rearrange("p (u a b e) -> p u a b e", u=2, b=8, e=2)
+                view = banks[pair][:].bitcast(BF16).rearrange("p (u n e) -> p u n e", u=2, e=2)
                 for t in range(4):
                     nc.scalar.activation(
-                        out=pl[:, :, t, :], in_=view[:, t // 2, :, :, t % 2], func=ACT.Copy,
+                        out=pl[:, t // 2, :, t % 2], in_=view[:, t // 2, :, t % 2], func=ACT.Copy,
                         scale=scale_col[:, 4 * S_PASS + t : 4 * S_PASS + t + 1],
                     )
 
@@ -236,11 +236,11 @@ def tile_attention_pa_kernel(tc, x, freqs_cis, wqkv_bytes, wqkv_scale, q_norm_w,
             gr = grouped_pool.tile([P, D], BF16, name="grouped_%d" % k, tag="grouped", align_bytes=64)
             grouped[k] = gr
             for pair in range(2):
-                for h in range(2):
+                for u in range(2):
                     nc.tensor.matmul(
-                        out=s_banks[g][pair][:].bitcast(BF16)[:, 512 * h : 512 * (h + 1)].rearrange("p (a b t) -> p a b t", b=8, t=4),
+                        out=s_banks[g][pair][:].bitcast(BF16).rearrange("p (n u e) -> p u n e", u=2, e=2)[:, u, :, :],
                         lhsT=ident_bf[:],
-                        rhs=planes[(g, pair)][:, 16 * h : 16 * (h + 1), :, :].rearrange("p a t b -> p a b t"),
+                        rhs=planes[(g, pair)][:, u, :, :],
                         start=True, stop=True,
                     )
             for pair in range(2):

from contextlib import ExitStack

import concourse.mybir as mybir
from concourse.masks import make_identity

FLOPS = 2 * 512 * 3072 * 2048

F32 = mybir.dt.float32
BF16 = mybir.dt.bfloat16
U32 = mybir.dt.uint32
U8 = mybir.dt.uint8
FP8 = mybir.dt.float8_e4m3fn
FP8X4 = mybir.dt.float8_e4m3fn_x4
ALU = mybir.AluOpType
ACT = mybir.ActivationFunctionType

P = 128
D = 2048
PASSES = 4
TOK_TILES = 4
ROW_TILES = 24
GROUPS = 6
ROPE_GROUPS = 5
UNITS = 4 + 4 * GROUPS
EPS = 1e-6
S_PASS = 3
S_GROUPS = (1, 2, 3, 4, 5)
V_CASTS = ()
S_CAST = (0, 1, 3, 11, 15, 19)
S_TURN = (0, 2, 9, 13, 17, 21)
S_QUANT = (0, 5, 11, 15, 19, 99)


def tile_attention_pa_kernel(tc, x, freqs_cis, wqkv_bytes, wqkv_scale, q_norm_w, k_norm_w, out_0, out_1, out_2):
    nc = tc.nc
    x_rows = x.rearrange("b s d -> (b s) d").rearrange("(m p) d -> p m d", p=P)
    outs = [
        out_0.rearrange("b s h d -> (b s) (h d)"),
        out_1.rearrange("b s h d -> (b s) (h d)"),
        out_2.rearrange("b s h d -> (b s) (h d)"),
    ]

    with ExitStack() as ctx:
        keep = ctx.enter_context(tc.tile_pool(name="keep", bufs=1))
        bytes_pool = ctx.enter_context(tc.tile_pool(name="bytes_pool", bufs=ROW_TILES))
        wide_pool = ctx.enter_context(tc.tile_pool(name="wide_pool", bufs=8))
        cast_pool = ctx.enter_context(tc.tile_pool(name="cast_pool", bufs=2))
        plane_pool = ctx.enter_context(tc.tile_pool(name="plane_pool", bufs=4))
        grouped_pool = ctx.enter_context(tc.tile_pool(name="grouped_pool", bufs=7))
        codes_pool = ctx.enter_context(tc.tile_pool(name="codes_pool", bufs=3))
        sum_pool = ctx.enter_context(tc.tile_pool(name="sum_pool", bufs=8))
        out_pool = ctx.enter_context(tc.tile_pool(name="out_pool", bufs=4))
        stat_pool = ctx.enter_context(tc.tile_pool(name="stat_pool", bufs=3))
        psum_t = ctx.enter_context(tc.psum_pool(name="psum_t", bufs=4))
        psum_acc = ctx.enter_context(tc.psum_pool(name="psum_acc", bufs=4))
        ctx.enter_context(tc.manual_schedule())

        scale_col = keep.tile([P, 16], F32, name="scale_col")
        nc.sync.dma_start(out=scale_col[:].rearrange("p (g t) -> p g t", t=4), in_=wqkv_scale.rearrange("o (g p t) -> p (o g) t", p=P, t=4))
        fc = keep.tile([P, 2, 64, 2], BF16, name="fc")
        nc.sync.dma_start(out=fc[:].rearrange("p t j e -> p t (j e)"), in_=freqs_cis.rearrange("(t p) j e -> p t (j e)", p=P))
        gain_col = []
        for name, vec in (("gain_col_q", q_norm_w), ("gain_col_k", k_norm_w)):
            g_c = keep.tile([P, 1], BF16, name=name)
            nc.scalar.dma_start(out=g_c[:], in_=vec.rearrange("(p o) -> p o", o=1))
            gain_col.append(g_c)

        w_bytes = {}
        x_raw = {}

        def load_w(t):
            wb = bytes_pool.tile([P, D], U8, name="w_bytes_%d" % t, tag="w_bytes")
            nc.sync.dma_start(out=wb[:], in_=wqkv_bytes[P * t : P * (t + 1), :])
            w_bytes[t] = wb

        def load_x(c):
            xr = wide_pool.tile([P, TOK_TILES, 512], BF16, name="x_raw_%d" % c, tag="wide")
            nc.sync.dma_start(out=xr[:], in_=x_rows[:, :, 512 * c : 512 * (c + 1)])
            x_raw[c] = xr

        load_w(0)
        load_x(0)
        load_w(1)
        load_x(1)
        for t in range(4, 8):
            load_w(t)
        load_w(2)
        load_x(2)
        load_w(3)
        load_x(3)
        for t in range(8, ROW_TILES):
            load_w(t)

        warm = keep.tile([P, 1], F32, name="warm")
        nc.gpsimd.memset(warm[:], 1.0)
        warm2 = keep.tile([P, 1], F32, name="warm2")
        nc.scalar.activation(out=warm2[:], in_=warm[:], func=ACT.Abs_reciprocal_sqrt)
        ident_bf = keep.tile([P, P], BF16, name="ident_bf")
        make_identity(nc, ident_bf[:])
        ident = keep.tile([P, P], F32, name="ident")
        make_identity(nc, ident[:])

        warm_ps = psum_t.tile([P, 512], F32, name="warm_ps", tag="tp")
        for i in range(14):
            nc.tensor.matmul(out=warm_ps[:, 0:P], lhsT=ident_bf[:], rhs=ident_bf[:], start=True, stop=True)

        gains_ps = psum_t.tile([P, 512], F32, name="gains_ps", tag="tp")
        gains = []
        for qk, name in enumerate(("gain_q", "gain_k")):
            nc.tensor.transpose(gains_ps[:].bitcast(BF16)[:, P * qk : P * (qk + 1)], gain_col[qk][:].to_broadcast([P, P]), ident_bf[:])
            g_t = keep.tile([P, 128], BF16, name=name)
            nc.scalar.copy(out=g_t[:], in_=gains_ps[:].bitcast(BF16)[:, P * qk : P * (qk + 1)])
            gains.append(g_t)
        fi_signed = keep.tile([P, 2, 2, 64], BF16, name="fi_signed")
        nc.scalar.copy(out=fi_signed[:, 0, :, :].unsqueeze(3), in_=fc[:, :, :, 1:2])
        nc.scalar.activation(out=fi_signed[:, 1, :, :].unsqueeze(3), in_=fc[:, :, :, 1:2], func=ACT.Copy, scale=-1.0)
        scale_b = keep.tile([P, D], F32, name="scale_b")
        for g in range(PASSES):
            sp = psum_t.tile([P, 512], F32, name="scale_ps_%d" % g, tag="tp")
            for t in range(4):
                nc.tensor.transpose(sp[:, P * t : P * (t + 1)], scale_col[:, 4 * g + t : 4 * g + t + 1].to_broadcast([P, P]), ident[:])
            nc.scalar.copy(
                out=scale_b[:, 512 * g : 512 * (g + 1)].rearrange("p (n t) -> p n t", t=4),
                in_=sp[:].rearrange("p (t n) -> p n t", t=4),
            )

        tab = []

        def tables():
            g4 = []
            for qk in range(2):
                g4.append(gains[qk][:].rearrange("p (j e) -> p j e", e=2).unsqueeze(1).to_broadcast([P, 2, 64, 2]))
            for qk in range(2):
                tab.append(keep.tile([P, 2, 2, 128], F32, name="tab_%d" % qk))
                nc.vector.tensor_tensor(
                    out=tab[qk][:, :, 0, :].rearrange("p t (j e) -> p t j e", e=2), in0=g4[qk],
                    in1=fc[:, :, :, 0:1].to_broadcast([P, 2, 64, 2]), op=ALU.mult,
                )
            for qk in range(2):
                nc.vector.tensor_tensor(
                    out=tab[qk][:, :, 1, :].rearrange("p t (j e) -> p t j e", e=2), in0=g4[qk],
                    in1=fi_signed[:].rearrange("p e t j -> p t j e"), op=ALU.mult,
                )

        tables()

        x_codes = keep.tile([P, PASSES, 512], U32, name="x_codes", align_bytes=64)
        x_scales = keep.tile([P, PASSES, 512], U8, name="x_scales", align_bytes=64)

        wide = {}
        grouped = {}
        w_codes = {}
        w_scales = {}
        acc = {}
        rope = {}
        sumsq = {}
        rstd = {}
        casts = {}
        dead = []
        planes = {}
        s_banks = {}
        sums = {}

        def widen(t):
            wd = wide_pool.tile([P, D], BF16, name="wide_%d" % t, tag="wide")
            last = 512 * S_PASS if t // 4 in S_GROUPS else D
            width = 512 if t == 0 else last
            for first in range(0, last, width):
                cols = slice(first, first + width)
                nc.vector.tensor_tensor(out=wd[:, cols], in0=w_bytes[t][:, cols].bitcast(FP8), in1=scale_b[:, cols], op=ALU.mult)
                dead.append(w_bytes[t][:, first + width - 1 : first + width])
            wide[t] = wd

        def widen_last(c):
            cols = slice(512 * c, 512 * (c + 1))
            for t in range(20, ROW_TILES):
                if c == 0:
                    wide[t] = wide_pool.tile([P, D], BF16, name="wide_%d" % t, tag="wide")
                nc.vector.tensor_tensor(out=wide[t][:, cols], in0=w_bytes[t][:, cols].bitcast(FP8), in1=scale_b[:, cols], op=ALU.mult)
                dead.append(w_bytes[t][:, 512 * c + 511 : 512 * (c + 1)])

        def cast(g, j):
            if j == 0:
                casts[g] = cast_pool.tile([P, 4, 512], BF16, name="cast_%d" % g, tag="cast")
            if g in V_CASTS:
                nc.vector.tensor_copy(out=casts[g][:, j, :], in_=w_bytes[4 * g + j][:, 512 * S_PASS : 512 * (S_PASS + 1)].bitcast(FP8))
                dead.append(w_bytes[4 * g + j][:, D - 1 : D])
            else:
                nc.scalar.copy(out=casts[g][:, j, :], in_=w_bytes[4 * g + j][:, 512 * S_PASS : 512 * (S_PASS + 1)].bitcast(FP8))

        def unit_words(k, j):
            if k < PASSES:
                return x_raw[k][:, j, :].bitcast(F32)
            g, p = divmod(k - PASSES, PASSES)
            if g in S_GROUPS and p == S_PASS:
                return casts[g][:, j, :].bitcast(F32)
            return wide[4 * g + j][:].bitcast(F32)[:, 256 * p : 256 * (p + 1)]

        def transposes(k):
            banks = []
            for pair in range(2):
                tp = psum_t.tile([P, 512], F32, name="tp_%d_%d" % (k, pair), tag="tp")
                banks.append(tp)
                for jj in range(2):
                    words = unit_words(k, 2 * pair + jj)
                    for u in range(2):
                        nc.tensor.transpose(tp[:, 256 * u + P * jj : 256 * u + P * (jj + 1)], words[:, u : 256 : 2], ident[:])
            return banks

        def turn(k):
            gr = grouped_pool.tile([P, D], BF16, name="grouped_%d" % k, tag="grouped", align_bytes=64)
            grouped[k] = gr
            banks = transposes(k)
            for pair in range(2):
                nc.scalar.copy(
                    out=gr[:, 1024 * pair : 1024 * (pair + 1)].bitcast(F32).rearrange("p (n u) -> p n u", u=2),
                    in_=banks[pair][:].rearrange("p (u n) -> p n u", u=2),
                )

        def turn_s(g):
            k = PASSES + PASSES * g + S_PASS
            banks = transposes(k)
            s_banks[g] = banks
            for pair in range(2):
                pl = plane_pool.tile([P, 2, 256, 2], BF16, name="planes_%d_%d" % (g, pair), tag="planes")
                planes[(g, pair)] = pl
                view = banks[pair][:].bitcast(BF16).rearrange("p (u n e) -> p u n e", u=2, e=2)
                for t in range(4):
                    nc.scalar.activation(
                        out=pl[:, t // 2, :, t % 2], in_=view[:, t // 2, :, t % 2], func=ACT.Copy,
                        scale=scale_col[:, 4 * S_PASS + t : 4 * S_PASS + t + 1],
                    )

        def stage_b(g):
            k = PASSES + PASSES * g + S_PASS
            gr = grouped_pool.tile([P, D], BF16, name="grouped_%d" % k, tag="grouped", align_bytes=64)
            grouped[k] = gr
            for pair in range(2):
                for u in range(2):
                    nc.tensor.matmul(
                        out=s_banks[g][pair][:].bitcast(BF16).rearrange("p (n u e) -> p u n e", u=2, e=2)[:, u, :, :],
                        lhsT=ident_bf[:],
                        rhs=planes[(g, pair)][:, u, :, :],
                        start=True, stop=True,
                    )
            for pair in range(2):
                nc.scalar.copy(out=gr[:, 1024 * pair : 1024 * (pair + 1)].bitcast(F32), in_=s_banks[g][pair][:])

        def quantize(k):
            if k < PASSES:
                codes, scales = x_codes[:, k, :], x_scales[:, k, :]
            else:
                g, p = divmod(k - PASSES, PASSES)
                for n in range(len(w_codes), g + 1):
                    w_codes[n] = codes_pool.tile([P, PASSES, 512], U32, name="w_codes_%d" % n, tag="w_codes", align_bytes=64)
                    w_scales[n] = codes_pool.tile([P, PASSES, 512], U8, name="w_scales_%d" % n, tag="w_scales", align_bytes=64)
                codes, scales = w_codes[g][:, p, :], w_scales[g][:, p, :]
            nc.vector.quantize_mx(out=codes.bitcast(FP8X4), scales=scales, in_=grouped[k][:])
            dead.append(grouped[k][:, 0:1])

        def multiply(g, m):
            if g < ROPE_GROUPS:
                a = psum_acc.tile([P, 512], F32, name="acc_%d_%d" % (g, m), tag="acc")
            else:
                a = psum_t.tile([P, 512], F32, name="acc_%d_%d" % (g, m), tag="tp")
            acc[(g, m)] = a
            for p in range(PASSES):
                nc.tensor.matmul_mx(
                    out=a[:],
                    lhsT=x_codes[:, p, P * m : P * (m + 1)].bitcast(FP8X4),
                    lhsT_scale=x_scales[:, p, P * m : P * (m + 1)],
                    rhs=w_codes[g][:, p, :].bitcast(FP8X4),
                    rhs_scale=w_scales[g][:, p, :],
                    start=(p == 0),
                    stop=(p == PASSES - 1),
                )

        def store(g, m, tile_ap):
            rows = slice(P * m, P * (m + 1))
            if g < 4:
                dst = outs[0][rows, 512 * g : 512 * (g + 1)]
            else:
                dst = outs[g - 3][rows, :]
            (nc.scalar if g == 5 else nc.sync).dma_start(out=dst, in_=tile_ap)

        def squares(g, m):
            if m == 0:
                sumsq[g] = stat_pool.tile([P, 16], F32, name="sumsq_%d" % g, tag="sumsq")
            for h in range(4):
                junk = stat_pool.tile([P, 128], F32, name="junk_%d_%d_%d" % (g, m, h), tag="junk")
                nc.scalar.activation(
                    out=junk[:], in_=acc[(g, m)][:, P * h : P * (h + 1)], func=ACT.Square,
                    accum_out=sumsq[g][:, 4 * m + h : 4 * m + h + 1],
                )

        def root(g, first, last):
            if first == 0:
                rstd[g] = stat_pool.tile([P, 16], F32, name="rstd_%d" % g, tag="rstd")
            cols = slice(4 * first, 4 * last)
            nc.scalar.activation(out=rstd[g][:, cols], in_=sumsq[g][:, cols], func=ACT.Abs_reciprocal_sqrt, scale=1.0 / 128.0, bias=EPS)

        def products(g, m):
            qk = 0 if g < 4 else 1
            t12 = sum_pool.tile([P, 2, 512], F32, name="t12_%d_%d" % (g, m), tag="t12")
            for h in range(4):
                head = slice(P * h, P * (h + 1))
                nc.vector.scalar_tensor_tensor(
                    out=t12[:, :, head],
                    in0=acc[(g, m)][:, head].unsqueeze(1).to_broadcast([P, 2, 128]),
                    scalar=rstd[g][:, 4 * m + h : 4 * m + h + 1],
                    in1=tab[qk][:, m % 2, :, :],
                    op0=ALU.mult, op1=ALU.mult,
                )
            rope[(g, m)] = t12

        def combine(engine, g, m):
            t12 = rope[(g, m)]
            engine.tensor_tensor(
                out=t12[:, 0, :].rearrange("p (n e) -> p n e", e=2),
                in0=t12[:, 0, :].rearrange("p (n e) -> p n e", e=2),
                in1=t12[:, 1, :].rearrange("p (n e) -> p n e", e=2)[:, :, ::-1],
                op=ALU.add,
            )
            store(g, m, t12[:, 0, :])

        def add_on_tensor(g, m):
            t12 = rope[(g, m)]
            ps = psum_t.tile([P, 512], F32, name="sum_%d_%d" % (g, m), tag="tp")
            nc.tensor.matmul(out=ps[:], lhsT=ident[:], rhs=t12[:, 0, :], start=True, stop=False)
            nc.tensor.matmul(
                out=ps[:].rearrange("p (n e) -> p n e", e=2), lhsT=ident[:],
                rhs=t12[:, 1, :].rearrange("p (n e) -> p n e", e=2)[:, :, ::-1], start=False, stop=True,
            )
            sums[(g, m)] = ps

        def burst(g, follow):
            late = {0: (), 4: ((3, 2), (3, 3))}.get(g, ((g - 1, 3),))
            if late:
                nc.gpsimd.memset(dead[-2], 0.0 if dead[-2].dtype == BF16 else 0)
            for bank in late:
                combine(nc.gpsimd, bank[0], bank[1])
            for m in range(TOK_TILES):
                products(g, m)
                if m < (1 if g == 4 else 2):
                    combine(nc.gpsimd, g, m)
                if follow is not None:
                    follow(m)
            if g < 3:
                combine(nc.vector, g, 2)

        def finish(g, m):
            o = out_pool.tile([P, 512], F32, name="o_%d_%d" % (g, m), tag="o")
            nc.scalar.copy(out=o[:], in_=sums[(g, m)][:])
            store(g, m, o[:])

        def plain_out(g, m):
            o = out_pool.tile([P, 512], F32, name="o_%d_%d" % (g, m), tag="o")
            nc.scalar.copy(out=o[:], in_=acc[(g, m)][:])
            store(g, m, o[:])

        def unit(g, p):
            return PASSES + PASSES * g + p

        def follow(g):
            def f(m):
                if m == 1 and g + 2 <= 5:
                    for p in range(2, PASSES):
                        if not (g + 2 in S_GROUPS and p == S_PASS):
                            turn(unit(g + 2, p))
                if 0 <= g + 1 < ROPE_GROUPS:
                    multiply(g + 1, m)
                    squares(g + 1, m)
                    if g + 1 == 4:
                        root(4, m, m + 1)
                    elif m == 3:
                        root(g + 1, 0, 4)
                if g + 3 >= 3 and g + 3 in S_GROUPS and g + 3 not in V_CASTS:
                    cast(g + 3, m)
            return f


        for tick in range(24):
            a, phase = divmod(tick - 3, 4)
            widen(tick)
            if tick in (1, 2):
                turn(2 * tick - 2)
                turn(2 * tick - 1)
            if tick in (3, 4):
                quantize(2 * tick - 6)
                quantize(2 * tick - 5)
            if tick == 7:
                quantize(unit(0, 3))
            for g in S_GROUPS:
                if S_TURN[g] + 1 == tick:
                    stage_b(g)
            if phase == 0 and 0 <= a <= 4:
                turn(unit(a, 0))
                turn(unit(a, 1))
                if a >= 2:
                    burst(a - 2, follow(a - 2))
                else:
                    for m in range(TOK_TILES):
                        follow(a - 2)(m)
            for g in S_GROUPS:
                if S_TURN[g] == tick:
                    turn_s(g)
            for g in S_GROUPS:
                if S_CAST[g] == tick and (g < 3 or g in V_CASTS):
                    for j in range(4):
                        cast(g, j)
            if a == 0:
                if phase == 2:
                    quantize(unit(1, S_PASS))
                    quantize(unit(0, 0))
                if phase == 3:
                    quantize(unit(0, 1))
                    quantize(unit(0, 2))
            elif phase > 0 and a > 0:
                quantize(unit(a, phase - 1))
            for g in S_GROUPS:
                if S_QUANT[g] == tick and g > 1:
                    quantize(unit(g, S_PASS))
            if tick == 23:
                turn(unit(5, 0))
                turn(unit(5, 1))
                burst(3, follow(3))
                for p in (0, S_PASS, 1, 2):
                    quantize(unit(5, p))
                for m in range(TOK_TILES):
                    multiply(5, m)
                    plain_out(5, m)
                burst(4, None)
                for m in range(1, TOK_TILES):
                    combine(nc.vector, 4, m)
